import numpy as np
import ml_dtypes


def mxq(x, axis, fmt="e4m3"):
    dtype, down = {"e4m3": (ml_dtypes.float8_e4m3fn, 7), "e5m2": (ml_dtypes.float8_e5m2, 14)}[fmt]
    v = np.moveaxis(np.asarray(x, np.float32).astype(ml_dtypes.bfloat16).astype(np.float64), axis, -1)
    blocks = v.reshape(v.shape[:-1] + (-1, 32))
    amax = np.abs(blocks).max(-1, keepdims=True)
    byte = np.maximum(np.where(amax > 0, np.frexp(amax)[1] - 1 + 127, 0) - down, 1)
    scale = np.exp2(byte - 127.0)
    codes = (blocks / scale).astype(np.float32).astype(dtype).astype(np.float64)
    return np.moveaxis((codes * scale).reshape(v.shape), -1, axis)


WIDE = False


def mx_kscale(k):
    if not WIDE:
        return np.ones(k)
    levels = np.array([20, -20, 10, -10, 0])
    a = np.random.permutation(np.resize(levels, k // 512 * 4)).reshape(k // 512, 4)
    idx = np.arange(k)
    return np.exp2(a[idx // 512, idx % 128 // 32])


BF16 = ml_dtypes.bfloat16


def bf(x):
    return np.asarray(x, np.float32).astype(BF16)


def f64(x):
    return np.asarray(x).astype(np.float64)


M, K, N = 4096, 1024, 1024

THRESHOLD = 0.05
EPS = 1e-6


def ternarize(weight):
    scale = np.maximum(np.mean(np.abs(weight)), EPS)
    t = THRESHOLD * scale
    return np.where(weight > t, 1.0, np.where(weight < -t, -1.0, 0.0))


def setup_inputs():
    bound = 1.0 / np.sqrt(K)
    s = mx_kscale(N)
    r = s / s.min()
    keep = np.where(r <= 4.0, 1.0, 2.0 ** -20)
    x = np.random.standard_normal((M, K)) * 4.0 / np.sqrt(K)
    weight = np.random.uniform(-bound, bound, (N, K)) * keep[:, None]
    bias = np.random.standard_normal(N) * 0.5
    g = np.random.standard_normal((M, N)) * np.exp2(np.random.randint(-12, 1, (M, 1))) * r[None, :]
    return {"x": bf(x), "weight": bf(weight), "bias": bf(bias), "grad_out": bf(g)}


def reference(x, weight, bias, grad_out):
    q = ternarize(f64(weight))
    return mxq(f64(grad_out), 1, "e5m2") @ mxq(q, 0, "e4m3")

@@ -1,0 +1,253 @@
+from contextlib import ExitStack
+
+import concourse.mybir as mybir
+from concourse.masks import make_identity
+
+F32 = mybir.dt.float32
+BF16 = mybir.dt.bfloat16
+U32 = mybir.dt.uint32
+U8 = mybir.dt.uint8
+I32 = mybir.dt.int32
+E4M3X4 = mybir.dt.float8_e4m3fn_x4
+E5M2X4 = mybir.dt.float8_e5m2_x4
+ALU = mybir.AluOpType
+ACTF = mybir.ActivationFunctionType
+AXIS = mybir.AxisListType
+
+P = 128
+M_TOK = 4096
+N_CON = 1024
+K_OUT = 1024
+FLOPS = 2 * M_TOK * N_CON * K_OUT
+BYTES = 2 * N_CON * K_OUT + 2 * M_TOK * N_CON + 4 * M_TOK * K_OUT
+
+GROUPS = 8
+ACT_COLS = 896
+
+
+def tile_bitlinear_t_kernel(tc, x, weight, bias, grad_out, out):
+    nc = tc.nc
+    with ExitStack() as ctx:
+        const = ctx.enter_context(tc.tile_pool(name="const", bufs=1))
+        g_pool = ctx.enter_context(tc.tile_pool(name="g_pool", bufs=6))
+        gg_pool = ctx.enter_context(tc.tile_pool(name="gg_pool", bufs=3))
+        gc_pool = ctx.enter_context(tc.tile_pool(name="gc_pool", bufs=8))
+        qw_pool = ctx.enter_context(tc.tile_pool(name="qw_pool", bufs=2))
+        st_pool = ctx.enter_context(tc.tile_pool(name="st_pool", bufs=7))
+        tp_pool = ctx.enter_context(tc.psum_pool(name="tp_pool", bufs=4))
+        mm_pool = ctx.enter_context(tc.psum_pool(name="mm_pool", bufs=4))
+        ctx.enter_context(tc.manual_schedule())
+
+        ident = const.tile([P, P], F32, name="ident")
+        ones = const.tile([P, P], F32, name="ones")
+        warm = const.tile([P, 1], F32, name="warm")
+        junk = const.tile([P, 1024], BF16, name="junk")
+        acc_s = const.tile([P, 4], F32, name="acc_s")
+        acc_v = const.tile([P, 4], F32, name="acc_v")
+        absv = const.tile([P, 2048], BF16, name="absv")
+        junkv = const.tile([P, 2048], BF16, name="junkv")
+        scl = const.tile([P, 1], F32, name="scl")
+        thr = const.tile([P, 1], F32, name="thr")
+        nthr = const.tile([P, 1], F32, name="nthr")
+        w_sb = [const.tile([P, 4096], BF16, name="w_sb%d" % g) for g in range(2)]
+        q_codes = const.tile([P, 2048], U32, name="q_codes", align_bytes=64)
+        q_scales = const.tile([P, 2048], U8, name="q_scales", align_bytes=64)
+
+        nc.vector.memset(warm[:], 0.0)
+        nc.scalar.activation(out=warm[:], in_=warm[:], func=ACTF.Abs)
+        nc.vector.memset(ones[:], 1.0)
+        make_identity(nc, ident[:])
+
+        g_sb = {}
+        gg = {}
+        gc = {}
+        gs = {}
+        bm = {}
+        qg = {}
+
+        def load_w(k):
+            nc.sync.dma_start(
+                out=w_sb[k // 2][:, (k % 2) * 2048 : (k % 2 + 1) * 2048],
+                in_=weight[256 * k : 256 * (k + 1), :].rearrange("(p e) c -> p (e c)", e=2),
+            )
+
+        def load_g(s):
+            g_sb[s] = g_pool.tile([P, 4096], BF16, name="g_sb%d" % s, tag="g_sb")
+            nc.sync.dma_start(
+                out=g_sb[s][:],
+                in_=grad_out[512 * s : 512 * (s + 1), :].rearrange("(p j) n -> p (j n)", j=4),
+            )
+
+        def abs_sum(k):
+            base = (k % 2) * 2048
+            nc.scalar.activation(
+                out=junk[:, 0:ACT_COLS],
+                in_=w_sb[k // 2][:, base : base + ACT_COLS],
+                func=ACTF.Abs,
+                accum_out=acc_s[:, k : k + 1],
+            )
+            nv = 2048 - ACT_COLS
+            nc.vector.tensor_scalar(
+                out=absv[:, 0:nv].bitcast(I32),
+                in0=w_sb[k // 2][:, base + ACT_COLS : base + 2048].bitcast(I32),
+                scalar1=0x7FFF7FFF, scalar2=None, op0=ALU.bitwise_and,
+            )
+            nc.vector.tensor_scalar(
+                out=junkv[:, 0:nv], in0=absv[:, 0:nv], scalar1=1.0, scalar2=None,
+                op0=ALU.mult, op1=ALU.add, accum_out=acc_v[:, k : k + 1],
+            )
+
+        def threshold():
+            ps = mm_pool.tile([P, 512], F32, name="ps_mean", tag="mm")
+            for k in range(4):
+                nc.tensor.matmul(out=ps[:, 0:1], lhsT=ones[:], rhs=acc_v[:, k : k + 1], start=(k == 0), stop=False)
+                nc.tensor.matmul(out=ps[:, 0:1], lhsT=ones[:], rhs=acc_s[:, k : k + 1], start=False, stop=(k == 3))
+            nc.vector.tensor_scalar(
+                out=scl[:], in0=ps[:, 0:1], scalar1=1.0 / (N_CON * K_OUT), scalar2=1e-6,
+                op0=ALU.mult, op1=ALU.max,
+            )
+            nc.vector.tensor_scalar(out=nthr[:], in0=scl[:], scalar1=-0.05, scalar2=None, op0=ALU.mult)
+            nc.vector.tensor_scalar(out=thr[:], in0=scl[:], scalar1=0.05, scalar2=None, op0=ALU.mult)
+
+        def w_view(g, h):
+            return w_sb[g][:].rearrange("p (t c) -> p t c", t=4)[:, :, h * 512 : (h + 1) * 512]
+
+        def ternary(g, h):
+            c = (g, h)
+            bm[c] = qw_pool.tile([P, 2048], BF16, name="bm%d%d" % c, tag="bm")
+            qg[c] = qw_pool.tile([P, 2048], BF16, name="qg%d%d" % c, tag="qg", align_bytes=64)
+            bview = bm[c][:].rearrange("p (t c) -> p t c", t=4)
+            nc.vector.tensor_scalar(
+                out=bview, in0=w_view(g, h), scalar1=nthr[:, 0:1], scalar2=None, op0=ALU.is_lt
+            )
+            nc.vector.scalar_tensor_tensor(
+                out=qg[c][:].rearrange("p (c t) -> p c t", t=4),
+                in0=w_view(g, h).rearrange("p t c -> p c t"),
+                scalar=thr[:, 0:1],
+                in1=bview.rearrange("p t c -> p c t"),
+                op0=ALU.is_gt,
+                op1=ALU.subtract,
+            )
+
+        def q_cols(g, h):
+            return slice(g * 1024 + h * 512, g * 1024 + (h + 1) * 512)
+
+        def quant_q(g, h):
+            nc.vector.quantize_mx(
+                out=q_codes[:, q_cols(g, h)].bitcast(E4M3X4),
+                scales=q_scales[:, q_cols(g, h)],
+                in_=qg[(g, h)][:],
+            )
+
+        def transposes(s, engines):
+            gg[s] = gg_pool.tile([P, 4096], BF16, name="gg%d" % s, tag="gg", align_bytes=64)
+            words = g_sb[s][:].bitcast(F32)
+            banks = []
+            for j in range(4):
+                tp = tp_pool.tile([P, 512], F32, name="tp%d_%d" % (s, j), tag="tp")
+                for k in range(4):
+                    nc.tensor.transpose(
+                        out=tp[:, k * 128 : (k + 1) * 128],
+                        in_=words[:, j * 512 + k * 128 : j * 512 + (k + 1) * 128],
+                        identity=ident[:],
+                    )
+                banks.append(tp)
+            for j in range(4):
+                dst = gg[s][:].bitcast(F32)[:, j * 512 : (j + 1) * 512].rearrange(
+                    "p (g m u) -> p g m u", g=2, u=2
+                )
+                src = banks[j][:].rearrange("p (g u m) -> p g m u", g=2, u=2)
+                if engines[j] == "s":
+                    nc.scalar.copy(out=dst, in_=src)
+                else:
+                    nc.vector.tensor_copy(out=dst, in_=src)
+
+        def quant_g(s):
+            gc[s] = gc_pool.tile([P, 1024], U32, name="gc%d" % s, tag="gc", align_bytes=64)
+            gs[s] = gc_pool.tile([P, 1024], U8, name="gs%d" % s, tag="gs", align_bytes=64)
+            nc.vector.quantize_mx(out=gc[s][:].bitcast(E5M2X4), scales=gs[s][:], in_=gg[s][:])
+
+        def unit(s, banks, dram, engines):
+            st = st_pool.tile([P, 2048], F32, name="st", tag="st")
+            for b in range(4):
+                j, h = banks[b]
+                ps = mm_pool.tile([P, 512], F32, name="ps", tag="mm")
+                for g in range(2):
+                    cols = slice(j * 256 + g * 128, j * 256 + (g + 1) * 128)
+                    nc.tensor.matmul_mx(
+                        out=ps[:],
+                        lhsT=gc[s][:, cols].bitcast(E5M2X4),
+                        lhsT_scale=gs[s][:, cols],
+                        rhs=q_codes[:, q_cols(g, h)].bitcast(E4M3X4),
+                        rhs_scale=q_scales[:, q_cols(g, h)],
+                        start=(g == 0),
+                        stop=(g == 1),
+                    )
+                dst = st[:, b * 512 : (b + 1) * 512]
+                if engines[b] == "s":
+                    nc.scalar.copy(out=dst, in_=ps[:])
+                else:
+                    nc.vector.tensor_copy(out=dst, in_=ps[:])
+            nc.sync.dma_start(out=dram, in_=st[:].rearrange("p (a k) -> p a k", a=dram.shape[1]))
+
+        def unit_half(s, h, engines):
+            rows = out[512 * s : 512 * (s + 1), h * 512 : (h + 1) * 512]
+            unit(s, [(j, h) for j in range(4)], rows.rearrange("(p j) k -> p j k", j=4), engines)
+
+        def unit_pair(s, a, engines):
+            rows = out[512 * s : 512 * (s + 1), :].rearrange("(p j) k -> p j k", j=4)
+            unit(
+                s,
+                [(2 * a, 0), (2 * a, 1), (2 * a + 1, 0), (2 * a + 1, 1)],
+                rows[:, 2 * a : 2 * a + 2, :],
+                engines,
+            )
+
+        for k in range(4):
+            load_w(k)
+        for s in range(6):
+            load_g(s)
+        for k in range(4):
+            abs_sum(k)
+        threshold()
+        transposes(0, "ssss")
+        load_g(6)
+        transposes(1, "ssss")
+        load_g(7)
+        ternary(0, 0)
+        ternary(1, 0)
+        quant_q(0, 0)
+        quant_q(1, 0)
+        transposes(2, "ssss")
+        quant_g(0)
+        transposes(3, "ssss")
+        quant_g(1)
+        unit_half(0, 0, "ssss")
+        quant_g(2)
+        unit_half(1, 0, "ssss")
+        transposes(4, "ssss")
+        ternary(0, 1)
+        ternary(1, 1)
+        quant_q(0, 1)
+        quant_q(1, 1)
+        unit_half(2, 0, "ssss")
+        transposes(5, "ssss")
+        quant_g(3)
+        unit_half(0, 1, "sssv")
+        unit_half(1, 1, "sssv")
+        transposes(6, "vvvv")
+        quant_g(4)
+        unit_half(2, 1, "sssv")
+        unit_pair(3, 0, "sssv")
+        transposes(7, "vvvv")
+        quant_g(5)
+        unit_pair(3, 1, "sssv")
+        unit_pair(4, 0, "sssv")
+        quant_g(6)
+        unit_pair(4, 1, "sssv")
+        unit_pair(5, 0, "sssv")
+        quant_g(7)
+        unit_pair(5, 1, "sssv")
+        for s in range(6, 8):
+            for a in range(2):
+                unit_pair(s, a, "svsv")

@@ -33,9 +33,9 @@ def tile_bitlinear_t_kernel(tc, x, weight, bias, grad_out, out):
         gg_pool = ctx.enter_context(tc.tile_pool(name="gg_pool", bufs=3))
         gc_pool = ctx.enter_context(tc.tile_pool(name="gc_pool", bufs=8))
         qw_pool = ctx.enter_context(tc.tile_pool(name="qw_pool", bufs=2))
-        st_pool = ctx.enter_context(tc.tile_pool(name="st_pool", bufs=7))
-        tp_pool = ctx.enter_context(tc.psum_pool(name="tp_pool", bufs=4))
-        mm_pool = ctx.enter_context(tc.psum_pool(name="mm_pool", bufs=4))
+        st_pool = ctx.enter_context(tc.tile_pool(name="st_pool", bufs=5))
+        s1_pool = ctx.enter_context(tc.tile_pool(name="s1_pool", bufs=6))
+        psum = ctx.enter_context(tc.psum_pool(name="psum", bufs=8))
         ctx.enter_context(tc.manual_schedule())
 
         ident = const.tile([P, P], F32, name="ident")
@@ -98,7 +98,7 @@ def tile_bitlinear_t_kernel(tc, x, weight, bias, grad_out, out):
             )
 
         def threshold():
-            ps = mm_pool.tile([P, 512], F32, name="ps_mean", tag="mm")
+            ps = psum.tile([P, 512], F32, name="ps_mean", tag="bank")
             for k in range(4):
                 nc.tensor.matmul(out=ps[:, 0:1], lhsT=ones[:], rhs=acc_v[:, k : k + 1], start=(k == 0), stop=False)
                 nc.tensor.matmul(out=ps[:, 0:1], lhsT=ones[:], rhs=acc_s[:, k : k + 1], start=False, stop=(k == 3))
@@ -144,7 +144,7 @@ def tile_bitlinear_t_kernel(tc, x, weight, bias, grad_out, out):
             words = g_sb[s][:].bitcast(F32)
             banks = []
             for j in range(4):
-                tp = tp_pool.tile([P, 512], F32, name="tp%d_%d" % (s, j), tag="tp")
+                tp = psum.tile([P, 512], F32, name="tp%d_%d" % (s, j), tag="bank")
                 for k in range(4):
                     nc.tensor.transpose(
                         out=tp[:, k * 128 : (k + 1) * 128],
@@ -168,10 +168,13 @@ def tile_bitlinear_t_kernel(tc, x, weight, bias, grad_out, out):
             nc.vector.quantize_mx(out=gc[s][:].bitcast(E5M2X4), scales=gs[s][:], in_=gg[s][:])
 
         def unit(s, banks, dram, engines):
-            st = st_pool.tile([P, 2048], F32, name="st", tag="st")
-            for b in range(4):
+            if len(banks) == 4:
+                st = st_pool.tile([P, 2048], F32, name="st", tag="st")
+            else:
+                st = s1_pool.tile([P, 1024], F32, name="s1", tag="s1")
+            for b in range(len(banks)):
                 j, h = banks[b]
-                ps = mm_pool.tile([P, 512], F32, name="ps", tag="mm")
+                ps = psum.tile([P, 512], F32, name="ps", tag="bank")
                 for g in range(2):
                     cols = slice(j * 256 + g * 128, j * 256 + (g + 1) * 128)
                     nc.tensor.matmul_mx(
@@ -202,6 +205,10 @@ def tile_bitlinear_t_kernel(tc, x, weight, bias, grad_out, out):
                 rows[:, 2 * a : 2 * a + 2, :],
                 engines,
             )
+
+        def unit_tile(s, j, engines):
+            rows = out[512 * s : 512 * (s + 1), :].rearrange("(p j) k -> p j k", j=4)
+            unit(s, [(j, 0), (j, 1)], rows[:, j : j + 1, :], engines)
 
         for k in range(4):
             load_w(k)
@@ -242,12 +249,16 @@ def tile_bitlinear_t_kernel(tc, x, weight, bias, grad_out, out):
         transposes(7, "vvvv")
         quant_g(5)
         unit_pair(3, 1, "sssv")
-        unit_pair(4, 0, "sssv")
+        unit_tile(4, 0, "sv")
+        unit_tile(4, 1, "sv")
         quant_g(6)
-        unit_pair(4, 1, "sssv")
-        unit_pair(5, 0, "sssv")
+        unit_tile(4, 2, "sv")
+        unit_tile(4, 3, "sv")
+        unit_tile(5, 0, "sv")
+        unit_tile(5, 1, "sv")
         quant_g(7)
-        unit_pair(5, 1, "sssv")
+        unit_tile(5, 2, "sv")
+        unit_tile(5, 3, "sv")
         for s in range(6, 8):
-            for a in range(2):
-                unit_pair(s, a, "svsv")
+            for j in range(4):
+                unit_tile(s, j, "sv")

@@ -40,6 +40,8 @@ def tile_bitlinear_t_kernel(tc, x, weight, bias, grad_out, out):
 
         ident = const.tile([P, P], F32, name="ident")
         ones = const.tile([P, P], F32, name="ones")
+        dm_l = const.tile([P, P], BF16, name="dm_l")
+        dm_r = const.tile([P, 512], BF16, name="dm_r")
         warm = const.tile([P, 1], F32, name="warm")
         junk = const.tile([P, 1024], BF16, name="junk")
         acc_s = const.tile([P, 4], F32, name="acc_s")
@@ -56,6 +58,8 @@ def tile_bitlinear_t_kernel(tc, x, weight, bias, grad_out, out):
         nc.vector.memset(warm[:], 0.0)
         nc.scalar.activation(out=warm[:], in_=warm[:], func=ACTF.Abs)
         nc.vector.memset(ones[:], 1.0)
+        nc.vector.memset(dm_l[:], 0.0)
+        nc.vector.memset(dm_r[:], 0.0)
         make_identity(nc, ident[:])
 
         g_sb = {}
@@ -97,11 +101,17 @@ def tile_bitlinear_t_kernel(tc, x, weight, bias, grad_out, out):
                 op0=ALU.mult, op1=ALU.add, accum_out=acc_v[:, k : k + 1],
             )
 
+        def keep_warm(n):
+            scr = psum.tile([P, 512], F32, name="scr", tag="bank")
+            for i in range(n):
+                nc.tensor.matmul(out=scr[:], lhsT=dm_l[:], rhs=dm_r[:], start=True, stop=True)
+
         def threshold():
             ps = psum.tile([P, 512], F32, name="ps_mean", tag="bank")
             for k in range(4):
                 nc.tensor.matmul(out=ps[:, 0:1], lhsT=ones[:], rhs=acc_v[:, k : k + 1], start=(k == 0), stop=False)
                 nc.tensor.matmul(out=ps[:, 0:1], lhsT=ones[:], rhs=acc_s[:, k : k + 1], start=False, stop=(k == 3))
+                keep_warm((3, 3, 2, 2)[k])
             nc.vector.tensor_scalar(
                 out=scl[:], in0=ps[:, 0:1], scalar1=1.0 / (N_CON * K_OUT), scalar2=1e-6,
                 op0=ALU.mult, op1=ALU.max,
@@ -218,14 +228,17 @@ def tile_bitlinear_t_kernel(tc, x, weight, bias, grad_out, out):
             abs_sum(k)
         threshold()
         transposes(0, "ssss")
+        keep_warm(3)
         load_g(6)
         transposes(1, "ssss")
+        keep_warm(3)
         load_g(7)
         ternary(0, 0)
         ternary(1, 0)
         quant_q(0, 0)
         quant_q(1, 0)
         transposes(2, "ssss")
+        keep_warm(3)
         quant_g(0)
         transposes(3, "ssss")
         quant_g(1)

@@ -31,7 +31,7 @@ def tile_bitlinear_t_kernel(tc, x, weight, bias, grad_out, out):
         const = ctx.enter_context(tc.tile_pool(name="const", bufs=1))
         g_pool = ctx.enter_context(tc.tile_pool(name="g_pool", bufs=6))
         gg_pool = ctx.enter_context(tc.tile_pool(name="gg_pool", bufs=3))
-        gc_pool = ctx.enter_context(tc.tile_pool(name="gc_pool", bufs=8))
+        gc_pool = ctx.enter_context(tc.tile_pool(name="gc_pool", bufs=6))
         qw_pool = ctx.enter_context(tc.tile_pool(name="qw_pool", bufs=2))
         st_pool = ctx.enter_context(tc.tile_pool(name="st_pool", bufs=5))
         s1_pool = ctx.enter_context(tc.tile_pool(name="s1_pool", bufs=6))
@@ -40,8 +40,6 @@ def tile_bitlinear_t_kernel(tc, x, weight, bias, grad_out, out):
 
         ident = const.tile([P, P], F32, name="ident")
         ones = const.tile([P, P], F32, name="ones")
-        dm_l = const.tile([P, P], BF16, name="dm_l")
-        dm_r = const.tile([P, 512], BF16, name="dm_r")
         warm = const.tile([P, 1], F32, name="warm")
         junk = const.tile([P, 1024], BF16, name="junk")
         acc_s = const.tile([P, 4], F32, name="acc_s")
@@ -52,14 +50,12 @@ def tile_bitlinear_t_kernel(tc, x, weight, bias, grad_out, out):
         thr = const.tile([P, 1], F32, name="thr")
         nthr = const.tile([P, 1], F32, name="nthr")
         w_sb = [const.tile([P, 4096], BF16, name="w_sb%d" % g) for g in range(2)]
-        q_codes = const.tile([P, 2048], U32, name="q_codes", align_bytes=64)
-        q_scales = const.tile([P, 2048], U8, name="q_scales", align_bytes=64)
+        q_codes = const.tile([P, 2048], U32, name="q_codes", align_bytes=256)
+        q_scales = const.tile([P, 2048], U8, name="q_scales", align_bytes=256)
 
         nc.vector.memset(warm[:], 0.0)
         nc.scalar.activation(out=warm[:], in_=warm[:], func=ACTF.Abs)
         nc.vector.memset(ones[:], 1.0)
-        nc.vector.memset(dm_l[:], 0.0)
-        nc.vector.memset(dm_r[:], 0.0)
         make_identity(nc, ident[:])
 
         g_sb = {}
@@ -101,17 +97,11 @@ def tile_bitlinear_t_kernel(tc, x, weight, bias, grad_out, out):
                 op0=ALU.mult, op1=ALU.add, accum_out=acc_v[:, k : k + 1],
             )
 
-        def keep_warm(n):
-            scr = psum.tile([P, 512], F32, name="scr", tag="bank")
-            for i in range(n):
-                nc.tensor.matmul(out=scr[:], lhsT=dm_l[:], rhs=dm_r[:], start=True, stop=True)
-
         def threshold():
             ps = psum.tile([P, 512], F32, name="ps_mean", tag="bank")
             for k in range(4):
                 nc.tensor.matmul(out=ps[:, 0:1], lhsT=ones[:], rhs=acc_v[:, k : k + 1], start=(k == 0), stop=False)
                 nc.tensor.matmul(out=ps[:, 0:1], lhsT=ones[:], rhs=acc_s[:, k : k + 1], start=False, stop=(k == 3))
-                keep_warm((3, 3, 2, 2)[k])
             nc.vector.tensor_scalar(
                 out=scl[:], in0=ps[:, 0:1], scalar1=1.0 / (N_CON * K_OUT), scalar2=1e-6,
                 op0=ALU.mult, op1=ALU.max,
@@ -173,9 +163,14 @@ def tile_bitlinear_t_kernel(tc, x, weight, bias, grad_out, out):
                     nc.vector.tensor_copy(out=dst, in_=src)
 
         def quant_g(s):
-            gc[s] = gc_pool.tile([P, 1024], U32, name="gc%d" % s, tag="gc", align_bytes=64)
-            gs[s] = gc_pool.tile([P, 1024], U8, name="gs%d" % s, tag="gs", align_bytes=64)
-            nc.vector.quantize_mx(out=gc[s][:].bitcast(E5M2X4), scales=gs[s][:], in_=gg[s][:])
+            gc[s] = gc_pool.tile([P, 48 + 1024], U32, name="gc%d" % s, tag="gc", align_bytes=256)
+            gs[s] = gc_pool.tile([P, 2048], U8, name="gs%d" % s, tag="gs", align_bytes=256)
+            for k in range(8):
+                nc.vector.quantize_mx(
+                    out=gc[s][:, 48 + 128 * k : 48 + 128 * (k + 1)].bitcast(E5M2X4),
+                    scales=gs[s][:, 256 * k : 256 * k + 128],
+                    in_=gg[s][:, 512 * k : 512 * (k + 1)],
+                )
 
         def unit(s, banks, dram, engines):
             if len(banks) == 4:
@@ -186,11 +181,11 @@ def tile_bitlinear_t_kernel(tc, x, weight, bias, grad_out, out):
                 j, h = banks[b]
                 ps = psum.tile([P, 512], F32, name="ps", tag="bank")
                 for g in range(2):
-                    cols = slice(j * 256 + g * 128, j * 256 + (g + 1) * 128)
+                    k = 2 * j + g
                     nc.tensor.matmul_mx(
                         out=ps[:],
-                        lhsT=gc[s][:, cols].bitcast(E5M2X4),
-                        lhsT_scale=gs[s][:, cols],
+                        lhsT=gc[s][:, 48 + 128 * k : 48 + 128 * (k + 1)].bitcast(E5M2X4),
+                        lhsT_scale=gs[s][:, 256 * k : 256 * k + 128],
                         rhs=q_codes[:, q_cols(g, h)].bitcast(E4M3X4),
                         rhs_scale=q_scales[:, q_cols(g, h)],
                         start=(g == 0),
@@ -228,17 +223,14 @@ def tile_bitlinear_t_kernel(tc, x, weight, bias, grad_out, out):
             abs_sum(k)
         threshold()
         transposes(0, "ssss")
-        keep_warm(3)
         load_g(6)
         transposes(1, "ssss")
-        keep_warm(3)
         load_g(7)
         ternary(0, 0)
         ternary(1, 0)
         quant_q(0, 0)
         quant_q(1, 0)
         transposes(2, "ssss")
-        keep_warm(3)
         quant_g(0)
         transposes(3, "ssss")
         quant_g(1)

@@ -46,7 +46,6 @@ def tile_bitlinear_t_kernel(tc, x, weight, bias, grad_out, out):
         acc_v = const.tile([P, 4], F32, name="acc_v")
         absv = const.tile([P, 2048], BF16, name="absv")
         junkv = const.tile([P, 2048], BF16, name="junkv")
-        scl = const.tile([P, 1], F32, name="scl")
         thr = const.tile([P, 1], F32, name="thr")
         nthr = const.tile([P, 1], F32, name="nthr")
         w_sb = [const.tile([P, 4096], BF16, name="w_sb%d" % g) for g in range(2)]
@@ -103,11 +102,13 @@ def tile_bitlinear_t_kernel(tc, x, weight, bias, grad_out, out):
                 nc.tensor.matmul(out=ps[:, 0:1], lhsT=ones[:], rhs=acc_v[:, k : k + 1], start=(k == 0), stop=False)
                 nc.tensor.matmul(out=ps[:, 0:1], lhsT=ones[:], rhs=acc_s[:, k : k + 1], start=False, stop=(k == 3))
             nc.vector.tensor_scalar(
-                out=scl[:], in0=ps[:, 0:1], scalar1=1.0 / (N_CON * K_OUT), scalar2=1e-6,
+                out=nthr[:], in0=ps[:, 0:1], scalar1=-0.05 / (N_CON * K_OUT), scalar2=-0.05 * 1e-6,
+                op0=ALU.mult, op1=ALU.min,
+            )
+            nc.vector.tensor_scalar(
+                out=thr[:], in0=ps[:, 0:1], scalar1=0.05 / (N_CON * K_OUT), scalar2=0.05 * 1e-6,
                 op0=ALU.mult, op1=ALU.max,
             )
-            nc.vector.tensor_scalar(out=nthr[:], in0=scl[:], scalar1=-0.05, scalar2=None, op0=ALU.mult)
-            nc.vector.tensor_scalar(out=thr[:], in0=scl[:], scalar1=0.05, scalar2=None, op0=ALU.mult)
 
         def w_view(g, h):
             return w_sb[g][:].rearrange("p (t c) -> p t c", t=4)[:, :, h * 512 : (h + 1) * 512]
@@ -238,22 +239,22 @@ def tile_bitlinear_t_kernel(tc, x, weight, bias, grad_out, out):
         quant_g(2)
         unit_half(1, 0, "ssss")
         transposes(4, "ssss")
+        transposes(5, "ssss")
         ternary(0, 1)
         ternary(1, 1)
         quant_q(0, 1)
         quant_q(1, 1)
         unit_half(2, 0, "ssss")
-        transposes(5, "ssss")
         quant_g(3)
+        quant_g(4)
         unit_half(0, 1, "sssv")
         unit_half(1, 1, "sssv")
-        transposes(6, "vvvv")
-        quant_g(4)
+        transposes(6, "svsv")
+        transposes(7, "svsv")
         unit_half(2, 1, "sssv")
-        unit_pair(3, 0, "sssv")
-        transposes(7, "vvvv")
         quant_g(5)
-        unit_pair(3, 1, "sssv")
+        for j in range(4):
+            unit_tile(3, j, "sv")
         unit_tile(4, 0, "sv")
         unit_tile(4, 1, "sv")
         quant_g(6)

@@ -5,31 +5,39 @@ from concourse.masks import make_identity
 
 F32 = mybir.dt.float32
 BF16 = mybir.dt.bfloat16
+I32 = mybir.dt.int32
 U32 = mybir.dt.uint32
 U8 = mybir.dt.uint8
-I32 = mybir.dt.int32
 E4M3X4 = mybir.dt.float8_e4m3fn_x4
 E5M2X4 = mybir.dt.float8_e5m2_x4
 ALU = mybir.AluOpType
 ACTF = mybir.ActivationFunctionType
-AXIS = mybir.AxisListType
 
 P = 128
-M_TOK = 4096
+TOKENS = 4096
 N_CON = 1024
 K_OUT = 1024
-FLOPS = 2 * M_TOK * N_CON * K_OUT
-BYTES = 2 * N_CON * K_OUT + 2 * M_TOK * N_CON + 4 * M_TOK * K_OUT
+THRESHOLD = 0.05
+EPS = 1e-6
 
-GROUPS = 8
-ACT_COLS = 896
+FLOPS = 2 * TOKENS * N_CON * K_OUT
+BYTES = 2 * N_CON * K_OUT + 2 * TOKENS * N_CON + 4 * TOKENS * K_OUT
+
+GROUPS = TOKENS // 512
+HALF = 512
+G_RESIDENT = 6
+
+SCALAR_SUM_COLS = 896
+
+CODE_PAD = 48
+SCALE_SLOT = 256
 
 
 def tile_bitlinear_t_kernel(tc, x, weight, bias, grad_out, out):
     nc = tc.nc
     with ExitStack() as ctx:
         const = ctx.enter_context(tc.tile_pool(name="const", bufs=1))
-        g_pool = ctx.enter_context(tc.tile_pool(name="g_pool", bufs=6))
+        g_pool = ctx.enter_context(tc.tile_pool(name="g_pool", bufs=G_RESIDENT))
         gg_pool = ctx.enter_context(tc.tile_pool(name="gg_pool", bufs=3))
         gc_pool = ctx.enter_context(tc.tile_pool(name="gc_pool", bufs=6))
         qw_pool = ctx.enter_context(tc.tile_pool(name="qw_pool", bufs=2))
@@ -41,16 +49,17 @@ def tile_bitlinear_t_kernel(tc, x, weight, bias, grad_out, out):
         ident = const.tile([P, P], F32, name="ident")
         ones = const.tile([P, P], F32, name="ones")
         warm = const.tile([P, 1], F32, name="warm")
-        junk = const.tile([P, 1024], BF16, name="junk")
-        acc_s = const.tile([P, 4], F32, name="acc_s")
-        acc_v = const.tile([P, 4], F32, name="acc_v")
-        absv = const.tile([P, 2048], BF16, name="absv")
-        junkv = const.tile([P, 2048], BF16, name="junkv")
+        abs_s = const.tile([P, 1024], BF16, name="abs_s")
+        sum_s = const.tile([P, 4], F32, name="sum_s")
+        sum_v = const.tile([P, 4], F32, name="sum_v")
+        abs_v = const.tile([P, 2048], BF16, name="abs_v")
+        copy_v = const.tile([P, 2048], BF16, name="copy_v")
+        scale = const.tile([P, 1], F32, name="scale")
         thr = const.tile([P, 1], F32, name="thr")
-        nthr = const.tile([P, 1], F32, name="nthr")
-        w_sb = [const.tile([P, 4096], BF16, name="w_sb%d" % g) for g in range(2)]
-        q_codes = const.tile([P, 2048], U32, name="q_codes", align_bytes=256)
-        q_scales = const.tile([P, 2048], U8, name="q_scales", align_bytes=256)
+        neg_thr = const.tile([P, 1], F32, name="neg_thr")
+        w_sb = [const.tile([P, 4 * K_OUT], BF16, name="w_sb%d" % g) for g in range(2)]
+        q_codes = const.tile([P, 2 * K_OUT], U32, name="q_codes", align_bytes=256)
+        q_scales = const.tile([P, 2 * K_OUT], U8, name="q_scales", align_bytes=256)
 
         nc.vector.memset(warm[:], 0.0)
         nc.scalar.activation(out=warm[:], in_=warm[:], func=ACTF.Abs)
@@ -58,20 +67,20 @@ def tile_bitlinear_t_kernel(tc, x, weight, bias, grad_out, out):
         make_identity(nc, ident[:])
 
         g_sb = {}
-        gg = {}
-        gc = {}
-        gs = {}
-        bm = {}
-        qg = {}
+        g_t = {}
+        g_codes = {}
+        g_scales = {}
+        below = {}
+        q_bf = {}
 
-        def load_w(k):
+        def load_weight(k):
             nc.sync.dma_start(
                 out=w_sb[k // 2][:, (k % 2) * 2048 : (k % 2 + 1) * 2048],
                 in_=weight[256 * k : 256 * (k + 1), :].rearrange("(p e) c -> p (e c)", e=2),
             )
 
-        def load_g(s):
-            g_sb[s] = g_pool.tile([P, 4096], BF16, name="g_sb%d" % s, tag="g_sb")
+        def load_tokens(s):
+            g_sb[s] = g_pool.tile([P, 4 * N_CON], BF16, name="g_sb%d" % s, tag="g_sb")
             nc.sync.dma_start(
                 out=g_sb[s][:],
                 in_=grad_out[512 * s : 512 * (s + 1), :].rearrange("(p j) n -> p (j n)", j=4),
@@ -80,191 +89,189 @@ def tile_bitlinear_t_kernel(tc, x, weight, bias, grad_out, out):
         def abs_sum(k):
             base = (k % 2) * 2048
             nc.scalar.activation(
-                out=junk[:, 0:ACT_COLS],
-                in_=w_sb[k // 2][:, base : base + ACT_COLS],
+                out=abs_s[:, 0:SCALAR_SUM_COLS],
+                in_=w_sb[k // 2][:, base : base + SCALAR_SUM_COLS],
                 func=ACTF.Abs,
-                accum_out=acc_s[:, k : k + 1],
+                accum_out=sum_s[:, k : k + 1],
             )
-            nv = 2048 - ACT_COLS
+            cols = 2048 - SCALAR_SUM_COLS
             nc.vector.tensor_scalar(
-                out=absv[:, 0:nv].bitcast(I32),
-                in0=w_sb[k // 2][:, base + ACT_COLS : base + 2048].bitcast(I32),
+                out=abs_v[:, 0:cols].bitcast(I32),
+                in0=w_sb[k // 2][:, base + SCALAR_SUM_COLS : base + 2048].bitcast(I32),
                 scalar1=0x7FFF7FFF, scalar2=None, op0=ALU.bitwise_and,
             )
             nc.vector.tensor_scalar(
-                out=junkv[:, 0:nv], in0=absv[:, 0:nv], scalar1=1.0, scalar2=None,
-                op0=ALU.mult, op1=ALU.add, accum_out=acc_v[:, k : k + 1],
+                out=copy_v[:, 0:cols], in0=abs_v[:, 0:cols], scalar1=1.0, scalar2=None,
+                op0=ALU.mult, op1=ALU.add, accum_out=sum_v[:, k : k + 1],
             )
 
         def threshold():
-            ps = psum.tile([P, 512], F32, name="ps_mean", tag="bank")
+            total = psum.tile([P, HALF], F32, name="total", tag="bank")
             for k in range(4):
-                nc.tensor.matmul(out=ps[:, 0:1], lhsT=ones[:], rhs=acc_v[:, k : k + 1], start=(k == 0), stop=False)
-                nc.tensor.matmul(out=ps[:, 0:1], lhsT=ones[:], rhs=acc_s[:, k : k + 1], start=False, stop=(k == 3))
+                nc.tensor.matmul(out=total[:, 0:1], lhsT=ones[:], rhs=sum_v[:, k : k + 1], start=(k == 0), stop=False)
+                nc.tensor.matmul(out=total[:, 0:1], lhsT=ones[:], rhs=sum_s[:, k : k + 1], start=False, stop=(k == 3))
             nc.vector.tensor_scalar(
-                out=nthr[:], in0=ps[:, 0:1], scalar1=-0.05 / (N_CON * K_OUT), scalar2=-0.05 * 1e-6,
-                op0=ALU.mult, op1=ALU.min,
-            )
-            nc.vector.tensor_scalar(
-                out=thr[:], in0=ps[:, 0:1], scalar1=0.05 / (N_CON * K_OUT), scalar2=0.05 * 1e-6,
+                out=scale[:], in0=total[:, 0:1], scalar1=1.0 / (N_CON * K_OUT), scalar2=EPS,
                 op0=ALU.mult, op1=ALU.max,
             )
+            nc.vector.tensor_scalar(out=neg_thr[:], in0=scale[:], scalar1=-THRESHOLD, scalar2=None, op0=ALU.mult)
+            nc.vector.tensor_scalar(out=thr[:], in0=scale[:], scalar1=THRESHOLD, scalar2=None, op0=ALU.mult)
 
-        def w_view(g, h):
-            return w_sb[g][:].rearrange("p (t c) -> p t c", t=4)[:, :, h * 512 : (h + 1) * 512]
+        def w_quarter(g, h):
+            return w_sb[g][:].rearrange("p (t c) -> p t c", t=4)[:, :, h * HALF : (h + 1) * HALF]
 
-        def ternary(g, h):
-            c = (g, h)
-            bm[c] = qw_pool.tile([P, 2048], BF16, name="bm%d%d" % c, tag="bm")
-            qg[c] = qw_pool.tile([P, 2048], BF16, name="qg%d%d" % c, tag="qg", align_bytes=64)
-            bview = bm[c][:].rearrange("p (t c) -> p t c", t=4)
+        def ternarise(g, h):
+            quarter = (g, h)
+            below[quarter] = qw_pool.tile([P, 4 * HALF], BF16, name="below%d%d" % quarter, tag="below")
+            q_bf[quarter] = qw_pool.tile([P, 4 * HALF], BF16, name="q_bf%d%d" % quarter, tag="q_bf", align_bytes=64)
+            below_tc = below[quarter][:].rearrange("p (t c) -> p t c", t=4)
             nc.vector.tensor_scalar(
-                out=bview, in0=w_view(g, h), scalar1=nthr[:, 0:1], scalar2=None, op0=ALU.is_lt
+                out=below_tc, in0=w_quarter(g, h), scalar1=neg_thr[:, 0:1], scalar2=None, op0=ALU.is_lt
             )
             nc.vector.scalar_tensor_tensor(
-                out=qg[c][:].rearrange("p (c t) -> p c t", t=4),
-                in0=w_view(g, h).rearrange("p t c -> p c t"),
+                out=q_bf[quarter][:].rearrange("p (c t) -> p c t", t=4),
+                in0=w_quarter(g, h).rearrange("p t c -> p c t"),
                 scalar=thr[:, 0:1],
-                in1=bview.rearrange("p t c -> p c t"),
+                in1=below_tc.rearrange("p t c -> p c t"),
                 op0=ALU.is_gt,
                 op1=ALU.subtract,
             )
 
         def q_cols(g, h):
-            return slice(g * 1024 + h * 512, g * 1024 + (h + 1) * 512)
+            return slice(g * K_OUT + h * HALF, g * K_OUT + (h + 1) * HALF)
 
-        def quant_q(g, h):
+        def quantise_q(g, h):
             nc.vector.quantize_mx(
                 out=q_codes[:, q_cols(g, h)].bitcast(E4M3X4),
                 scales=q_scales[:, q_cols(g, h)],
-                in_=qg[(g, h)][:],
+                in_=q_bf[(g, h)][:],
             )
 
-        def transposes(s, engines):
-            gg[s] = gg_pool.tile([P, 4096], BF16, name="gg%d" % s, tag="gg", align_bytes=64)
+        def copy_out(on_scalar, dst, src):
+            if on_scalar:
+                nc.scalar.copy(out=dst, in_=src)
+            else:
+                nc.vector.tensor_copy(out=dst, in_=src)
+
+        def transposes(s, on_scalar):
+            g_t[s] = gg_pool.tile([P, 4 * N_CON], BF16, name="g_t%d" % s, tag="g_t", align_bytes=64)
             words = g_sb[s][:].bitcast(F32)
             banks = []
             for j in range(4):
-                tp = psum.tile([P, 512], F32, name="tp%d_%d" % (s, j), tag="bank")
+                bank = psum.tile([P, HALF], F32, name="tp%d_%d" % (s, j), tag="bank")
                 for k in range(4):
                     nc.tensor.transpose(
-                        out=tp[:, k * 128 : (k + 1) * 128],
+                        out=bank[:, k * 128 : (k + 1) * 128],
                         in_=words[:, j * 512 + k * 128 : j * 512 + (k + 1) * 128],
                         identity=ident[:],
                     )
-                banks.append(tp)
+                banks.append(bank)
             for j in range(4):
-                dst = gg[s][:].bitcast(F32)[:, j * 512 : (j + 1) * 512].rearrange(
-                    "p (g m u) -> p g m u", g=2, u=2
+                copy_out(
+                    on_scalar,
+                    g_t[s][:].bitcast(F32)[:, j * 512 : (j + 1) * 512].rearrange("p (g m u) -> p g m u", g=2, u=2),
+                    banks[j][:].rearrange("p (g u m) -> p g m u", g=2, u=2),
                 )
-                src = banks[j][:].rearrange("p (g u m) -> p g m u", g=2, u=2)
-                if engines[j] == "s":
-                    nc.scalar.copy(out=dst, in_=src)
-                else:
-                    nc.vector.tensor_copy(out=dst, in_=src)
 
-        def quant_g(s):
-            gc[s] = gc_pool.tile([P, 48 + 1024], U32, name="gc%d" % s, tag="gc", align_bytes=256)
-            gs[s] = gc_pool.tile([P, 2048], U8, name="gs%d" % s, tag="gs", align_bytes=256)
-            for k in range(8):
+        def code_cols(i):
+            return slice(CODE_PAD + 128 * i, CODE_PAD + 128 * (i + 1))
+
+        def scale_cols(i):
+            return slice(SCALE_SLOT * i, SCALE_SLOT * i + 128)
+
+        def quantise_tokens(s):
+            g_codes[s] = gc_pool.tile([P, CODE_PAD + 1024], U32, name="g_codes%d" % s, tag="g_codes", align_bytes=256)
+            g_scales[s] = gc_pool.tile([P, 8 * SCALE_SLOT], U8, name="g_scales%d" % s, tag="g_scales", align_bytes=256)
+            for i in range(8):
                 nc.vector.quantize_mx(
-                    out=gc[s][:, 48 + 128 * k : 48 + 128 * (k + 1)].bitcast(E5M2X4),
-                    scales=gs[s][:, 256 * k : 256 * k + 128],
-                    in_=gg[s][:, 512 * k : 512 * (k + 1)],
+                    out=g_codes[s][:, code_cols(i)].bitcast(E5M2X4),
+                    scales=g_scales[s][:, scale_cols(i)],
+                    in_=g_t[s][:, 512 * i : 512 * (i + 1)],
                 )
 
-        def unit(s, banks, dram, engines):
+        def products(s, banks, dram, scalar_banks):
             if len(banks) == 4:
-                st = st_pool.tile([P, 2048], F32, name="st", tag="st")
+                staged = st_pool.tile([P, 4 * HALF], F32, name="staged4", tag="staged4")
             else:
-                st = s1_pool.tile([P, 1024], F32, name="s1", tag="s1")
+                staged = s1_pool.tile([P, 2 * HALF], F32, name="staged2", tag="staged2")
             for b in range(len(banks)):
                 j, h = banks[b]
-                ps = psum.tile([P, 512], F32, name="ps", tag="bank")
+                acc = psum.tile([P, HALF], F32, name="acc", tag="bank")
                 for g in range(2):
-                    k = 2 * j + g
                     nc.tensor.matmul_mx(
-                        out=ps[:],
-                        lhsT=gc[s][:, 48 + 128 * k : 48 + 128 * (k + 1)].bitcast(E5M2X4),
-                        lhsT_scale=gs[s][:, 256 * k : 256 * k + 128],
+                        out=acc[:],
+                        lhsT=g_codes[s][:, code_cols(2 * j + g)].bitcast(E5M2X4),
+                        lhsT_scale=g_scales[s][:, scale_cols(2 * j + g)],
                         rhs=q_codes[:, q_cols(g, h)].bitcast(E4M3X4),
                         rhs_scale=q_scales[:, q_cols(g, h)],
                         start=(g == 0),
                         stop=(g == 1),
                     )
-                dst = st[:, b * 512 : (b + 1) * 512]
-                if engines[b] == "s":
-                    nc.scalar.copy(out=dst, in_=ps[:])
-                else:
-                    nc.vector.tensor_copy(out=dst, in_=ps[:])
-            nc.sync.dma_start(out=dram, in_=st[:].rearrange("p (a k) -> p a k", a=dram.shape[1]))
+                copy_out(b < scalar_banks, staged[:, b * HALF : (b + 1) * HALF], acc[:])
+            nc.sync.dma_start(out=dram, in_=staged[:].rearrange("p (a k) -> p a k", a=dram.shape[1]))
 
-        def unit_half(s, h, engines):
-            rows = out[512 * s : 512 * (s + 1), h * 512 : (h + 1) * 512]
-            unit(s, [(j, h) for j in range(4)], rows.rearrange("(p j) k -> p j k", j=4), engines)
+        def group_rows(s):
+            return out[512 * s : 512 * (s + 1), :].rearrange("(p j) k -> p j k", j=4)
 
-        def unit_pair(s, a, engines):
-            rows = out[512 * s : 512 * (s + 1), :].rearrange("(p j) k -> p j k", j=4)
-            unit(
+        def half_of_group(s, h, scalar_banks):
+            products(s, [(j, h) for j in range(4)], group_rows(s)[:, :, h * HALF : (h + 1) * HALF], scalar_banks)
+
+        def pair_of_tiles(s, a, scalar_banks):
+            products(
                 s,
                 [(2 * a, 0), (2 * a, 1), (2 * a + 1, 0), (2 * a + 1, 1)],
-                rows[:, 2 * a : 2 * a + 2, :],
-                engines,
+                group_rows(s)[:, 2 * a : 2 * a + 2, :],
+                scalar_banks,
             )
 
-        def unit_tile(s, j, engines):
-            rows = out[512 * s : 512 * (s + 1), :].rearrange("(p j) k -> p j k", j=4)
-            unit(s, [(j, 0), (j, 1)], rows[:, j : j + 1, :], engines)
+        def one_tile(s, j):
+            products(s, [(j, 0), (j, 1)], group_rows(s)[:, j : j + 1, :], 1)
 
         for k in range(4):
-            load_w(k)
-        for s in range(6):
-            load_g(s)
+            load_weight(k)
+        for s in range(G_RESIDENT):
+            load_tokens(s)
         for k in range(4):
             abs_sum(k)
         threshold()
-        transposes(0, "ssss")
-        load_g(6)
-        transposes(1, "ssss")
-        load_g(7)
-        ternary(0, 0)
-        ternary(1, 0)
-        quant_q(0, 0)
-        quant_q(1, 0)
-        transposes(2, "ssss")
-        quant_g(0)
-        transposes(3, "ssss")
-        quant_g(1)
-        unit_half(0, 0, "ssss")
-        quant_g(2)
-        unit_half(1, 0, "ssss")
-        transposes(4, "ssss")
-        transposes(5, "ssss")
-        ternary(0, 1)
-        ternary(1, 1)
-        quant_q(0, 1)
-        quant_q(1, 1)
-        unit_half(2, 0, "ssss")
-        quant_g(3)
-        quant_g(4)
-        unit_half(0, 1, "sssv")
-        unit_half(1, 1, "sssv")
-        transposes(6, "svsv")
-        transposes(7, "svsv")
-        unit_half(2, 1, "sssv")
-        quant_g(5)
-        for j in range(4):
-            unit_tile(3, j, "sv")
-        unit_tile(4, 0, "sv")
-        unit_tile(4, 1, "sv")
-        quant_g(6)
-        unit_tile(4, 2, "sv")
-        unit_tile(4, 3, "sv")
-        unit_tile(5, 0, "sv")
-        unit_tile(5, 1, "sv")
-        quant_g(7)
-        unit_tile(5, 2, "sv")
-        unit_tile(5, 3, "sv")
-        for s in range(6, 8):
+
+        transposes(0, True)
+        load_tokens(6)
+        transposes(1, True)
+        load_tokens(7)
+        ternarise(0, 0)
+        ternarise(1, 0)
+        quantise_q(0, 0)
+        quantise_q(1, 0)
+        transposes(2, True)
+        quantise_tokens(0)
+        transposes(3, True)
+        quantise_tokens(1)
+
+        half_of_group(0, 0, 4)
+        quantise_tokens(2)
+        half_of_group(1, 0, 4)
+        transposes(4, True)
+        ternarise(0, 1)
+        ternarise(1, 1)
+        quantise_q(0, 1)
+        quantise_q(1, 1)
+        half_of_group(2, 0, 4)
+        transposes(5, True)
+        quantise_tokens(3)
+
+        half_of_group(0, 1, 3)
+        half_of_group(1, 1, 3)
+        transposes(6, False)
+        quantise_tokens(4)
+        half_of_group(2, 1, 3)
+        pair_of_tiles(3, 0, 3)
+        transposes(7, False)
+        quantise_tokens(5)
+        pair_of_tiles(3, 1, 3)
+
+        for s in range(4, GROUPS):
             for j in range(4):
-                unit_tile(s, j, "sv")
+                one_tile(s, j)
+                if j == 1 and s + 2 < GROUPS:
+                    quantise_tokens(s + 2)

@@ -54,7 +54,6 @@ def tile_bitlinear_t_kernel(tc, x, weight, bias, grad_out, out):
         sum_v = const.tile([P, 4], F32, name="sum_v")
         abs_v = const.tile([P, 2048], BF16, name="abs_v")
         copy_v = const.tile([P, 2048], BF16, name="copy_v")
-        scale = const.tile([P, 1], F32, name="scale")
         thr = const.tile([P, 1], F32, name="thr")
         neg_thr = const.tile([P, 1], F32, name="neg_thr")
         w_sb = [const.tile([P, 4 * K_OUT], BF16, name="w_sb%d" % g) for g in range(2)]
@@ -110,32 +109,44 @@ def tile_bitlinear_t_kernel(tc, x, weight, bias, grad_out, out):
             for k in range(4):
                 nc.tensor.matmul(out=total[:, 0:1], lhsT=ones[:], rhs=sum_v[:, k : k + 1], start=(k == 0), stop=False)
                 nc.tensor.matmul(out=total[:, 0:1], lhsT=ones[:], rhs=sum_s[:, k : k + 1], start=False, stop=(k == 3))
+            per_element = THRESHOLD / (N_CON * K_OUT)
             nc.vector.tensor_scalar(
-                out=scale[:], in0=total[:, 0:1], scalar1=1.0 / (N_CON * K_OUT), scalar2=EPS,
+                out=neg_thr[:], in0=total[:, 0:1], scalar1=-per_element, scalar2=-THRESHOLD * EPS,
+                op0=ALU.mult, op1=ALU.min,
+            )
+            nc.vector.tensor_scalar(
+                out=thr[:], in0=total[:, 0:1], scalar1=per_element, scalar2=THRESHOLD * EPS,
                 op0=ALU.mult, op1=ALU.max,
             )
-            nc.vector.tensor_scalar(out=neg_thr[:], in0=scale[:], scalar1=-THRESHOLD, scalar2=None, op0=ALU.mult)
-            nc.vector.tensor_scalar(out=thr[:], in0=scale[:], scalar1=THRESHOLD, scalar2=None, op0=ALU.mult)
 
         def w_quarter(g, h):
             return w_sb[g][:].rearrange("p (t c) -> p t c", t=4)[:, :, h * HALF : (h + 1) * HALF]
 
-        def ternarise(g, h):
-            quarter = (g, h)
-            below[quarter] = qw_pool.tile([P, 4 * HALF], BF16, name="below%d%d" % quarter, tag="below")
-            q_bf[quarter] = qw_pool.tile([P, 4 * HALF], BF16, name="q_bf%d%d" % quarter, tag="q_bf", align_bytes=64)
-            below_tc = below[quarter][:].rearrange("p (t c) -> p t c", t=4)
+        def mark_below(g, h):
+            below[(g, h)] = qw_pool.tile([P, 4 * HALF], BF16, name="below%d%d" % (g, h), tag="below")
             nc.vector.tensor_scalar(
-                out=below_tc, in0=w_quarter(g, h), scalar1=neg_thr[:, 0:1], scalar2=None, op0=ALU.is_lt
+                out=below[(g, h)][:].rearrange("p (t c) -> p t c", t=4),
+                in0=w_quarter(g, h), scalar1=neg_thr[:, 0:1], scalar2=None, op0=ALU.is_lt,
             )
+
+        def ternarise(g, h):
+            q_bf[(g, h)] = qw_pool.tile([P, 4 * HALF], BF16, name="q_bf%d%d" % (g, h), tag="q_bf", align_bytes=64)
             nc.vector.scalar_tensor_tensor(
-                out=q_bf[quarter][:].rearrange("p (c t) -> p c t", t=4),
+                out=q_bf[(g, h)][:].rearrange("p (c t) -> p c t", t=4),
                 in0=w_quarter(g, h).rearrange("p t c -> p c t"),
                 scalar=thr[:, 0:1],
-                in1=below_tc.rearrange("p t c -> p c t"),
+                in1=below[(g, h)][:].rearrange("p (t c) -> p c t", t=4),
                 op0=ALU.is_gt,
                 op1=ALU.subtract,
             )
+
+        def build_half_of_q(h):
+            mark_below(0, h)
+            mark_below(1, h)
+            ternarise(0, h)
+            ternarise(1, h)
+            quantise_q(0, h)
+            quantise_q(1, h)
 
         def q_cols(g, h):
             return slice(g * K_OUT + h * HALF, g * K_OUT + (h + 1) * HALF)
@@ -216,16 +227,8 @@ def tile_bitlinear_t_kernel(tc, x, weight, bias, grad_out, out):
         def half_of_group(s, h, scalar_banks):
             products(s, [(j, h) for j in range(4)], group_rows(s)[:, :, h * HALF : (h + 1) * HALF], scalar_banks)
 
-        def pair_of_tiles(s, a, scalar_banks):
-            products(
-                s,
-                [(2 * a, 0), (2 * a, 1), (2 * a + 1, 0), (2 * a + 1, 1)],
-                group_rows(s)[:, 2 * a : 2 * a + 2, :],
-                scalar_banks,
-            )
-
-        def one_tile(s, j):
-            products(s, [(j, 0), (j, 1)], group_rows(s)[:, j : j + 1, :], 1)
+        def one_tile(s, j, scalar_banks):
+            products(s, [(j, 0), (j, 1)], group_rows(s)[:, j : j + 1, :], scalar_banks)
 
         for k in range(4):
             load_weight(k)
@@ -239,10 +242,7 @@ def tile_bitlinear_t_kernel(tc, x, weight, bias, grad_out, out):
         load_tokens(6)
         transposes(1, True)
         load_tokens(7)
-        ternarise(0, 0)
-        ternarise(1, 0)
-        quantise_q(0, 0)
-        quantise_q(1, 0)
+        build_half_of_q(0)
         transposes(2, True)
         quantise_tokens(0)
         transposes(3, True)
@@ -252,10 +252,7 @@ def tile_bitlinear_t_kernel(tc, x, weight, bias, grad_out, out):
         quantise_tokens(2)
         half_of_group(1, 0, 4)
         transposes(4, True)
-        ternarise(0, 1)
-        ternarise(1, 1)
-        quantise_q(0, 1)
-        quantise_q(1, 1)
+        build_half_of_q(1)
         half_of_group(2, 0, 4)
         transposes(5, True)
         quantise_tokens(3)
@@ -265,13 +262,15 @@ def tile_bitlinear_t_kernel(tc, x, weight, bias, grad_out, out):
         transposes(6, False)
         quantise_tokens(4)
         half_of_group(2, 1, 3)
-        pair_of_tiles(3, 0, 3)
+        one_tile(3, 0, 2)
+        one_tile(3, 1, 1)
         transposes(7, False)
         quantise_tokens(5)
-        pair_of_tiles(3, 1, 3)
+        one_tile(3, 2, 2)
+        one_tile(3, 3, 1)
 
         for s in range(4, GROUPS):
             for j in range(4):
-                one_tile(s, j)
+                one_tile(s, j, 1)
                 if j == 1 and s + 2 < GROUPS:
                     quantise_tokens(s + 2)

@@ -184,45 +184,45 @@ def tile_bitlinear_t_kernel(tc, x, weight, bias, grad_out, out):
                     banks[j][:].rearrange("p (g u m) -> p g m u", g=2, u=2),
                 )
 
-        def code_cols(i):
-            return slice(CODE_PAD + 128 * i, CODE_PAD + 128 * (i + 1))
+        def code_cols(j, g):
+            return slice(CODE_PAD + 128 * (2 * j + g), CODE_PAD + 128 * (2 * j + g + 1))
 
-        def scale_cols(i):
-            return slice(SCALE_SLOT * i, SCALE_SLOT * i + 128)
+        def scale_cols(j, g):
+            return slice(SCALE_SLOT * (2 * j + g), SCALE_SLOT * (2 * j + g) + 128)
 
         def quantise_tokens(s):
             g_codes[s] = gc_pool.tile([P, CODE_PAD + 1024], U32, name="g_codes%d" % s, tag="g_codes", align_bytes=256)
             g_scales[s] = gc_pool.tile([P, 8 * SCALE_SLOT], U8, name="g_scales%d" % s, tag="g_scales", align_bytes=256)
-            for i in range(8):
-                nc.vector.quantize_mx(
-                    out=g_codes[s][:, code_cols(i)].bitcast(E5M2X4),
-                    scales=g_scales[s][:, scale_cols(i)],
-                    in_=g_t[s][:, 512 * i : 512 * (i + 1)],
-                )
+            for j in range(4):
+                for g in range(2):
+                    nc.vector.quantize_mx(
+                        out=g_codes[s][:, code_cols(j, g)].bitcast(E5M2X4),
+                        scales=g_scales[s][:, scale_cols(j, g)],
+                        in_=g_t[s][:, 512 * (2 * j + g) : 512 * (2 * j + g + 1)],
+                    )
 
-        def products(s, banks, dram, scalar_banks):
-            if len(banks) == 4:
+        def products(s, parts, dram, scalar_banks):
+            if len(parts) == 4:
                 staged = st_pool.tile([P, 4 * HALF], F32, name="staged4", tag="staged4")
             else:
                 staged = s1_pool.tile([P, 2 * HALF], F32, name="staged2", tag="staged2")
-            for b in range(len(banks)):
-                j, h = banks[b]
+            for i, (j, h) in enumerate(parts):
                 acc = psum.tile([P, HALF], F32, name="acc", tag="bank")
                 for g in range(2):
                     nc.tensor.matmul_mx(
                         out=acc[:],
-                        lhsT=g_codes[s][:, code_cols(2 * j + g)].bitcast(E5M2X4),
-                        lhsT_scale=g_scales[s][:, scale_cols(2 * j + g)],
+                        lhsT=g_codes[s][:, code_cols(j, g)].bitcast(E5M2X4),
+                        lhsT_scale=g_scales[s][:, scale_cols(j, g)],
                         rhs=q_codes[:, q_cols(g, h)].bitcast(E4M3X4),
                         rhs_scale=q_scales[:, q_cols(g, h)],
                         start=(g == 0),
                         stop=(g == 1),
                     )
-                copy_out(b < scalar_banks, staged[:, b * HALF : (b + 1) * HALF], acc[:])
-            nc.sync.dma_start(out=dram, in_=staged[:].rearrange("p (a k) -> p a k", a=dram.shape[1]))
+                copy_out(i < scalar_banks, staged[:, i * HALF : (i + 1) * HALF], acc[:])
+            nc.sync.dma_start(out=dram, in_=staged[:].rearrange("p (r c) -> p r c", r=dram.shape[1]))
 
         def group_rows(s):
-            return out[512 * s : 512 * (s + 1), :].rearrange("(p j) k -> p j k", j=4)
+            return out[512 * s : 512 * (s + 1), :].rearrange("(p j) c -> p j c", j=4)
 
         def half_of_group(s, h, scalar_banks):
             products(s, [(j, h) for j in range(4)], group_rows(s)[:, :, h * HALF : (h + 1) * HALF], scalar_banks)
@@ -253,8 +253,8 @@ def tile_bitlinear_t_kernel(tc, x, weight, bias, grad_out, out):
         half_of_group(1, 0, 4)
         transposes(4, True)
         build_half_of_q(1)
-        half_of_group(2, 0, 4)
-        transposes(5, True)
+        half_of_group(2, 0, 3)
+        transposes(5, False)
         quantise_tokens(3)
 
         half_of_group(0, 1, 3)

@@ -27,7 +27,9 @@ GROUPS = TOKENS // 512
 HALF = 512
 G_RESIDENT = 6
 
-SCALAR_SUM_COLS = 896
+ABS_BITS = 0x7FFF7FFF
+SIGN_BITS = -0x7FFF8000
+ONE_BITS = 0x3F803F80
 
 CODE_PAD = 48
 SCALE_SLOT = 256
@@ -41,7 +43,7 @@ def tile_bitlinear_t_kernel(tc, x, weight, bias, grad_out, out):
         gg_pool = ctx.enter_context(tc.tile_pool(name="gg_pool", bufs=3))
         gc_pool = ctx.enter_context(tc.tile_pool(name="gc_pool", bufs=6))
         qw_pool = ctx.enter_context(tc.tile_pool(name="qw_pool", bufs=2))
-        st_pool = ctx.enter_context(tc.tile_pool(name="st_pool", bufs=5))
+        st_pool = ctx.enter_context(tc.tile_pool(name="st_pool", bufs=4))
         s1_pool = ctx.enter_context(tc.tile_pool(name="s1_pool", bufs=6))
         psum = ctx.enter_context(tc.psum_pool(name="psum", bufs=8))
         ctx.enter_context(tc.manual_schedule())
@@ -49,19 +51,18 @@ def tile_bitlinear_t_kernel(tc, x, weight, bias, grad_out, out):
         ident = const.tile([P, P], F32, name="ident")
         ones = const.tile([P, P], F32, name="ones")
         warm = const.tile([P, 1], F32, name="warm")
-        abs_s = const.tile([P, 1024], BF16, name="abs_s")
-        sum_s = const.tile([P, 4], F32, name="sum_s")
-        sum_v = const.tile([P, 4], F32, name="sum_v")
-        abs_v = const.tile([P, 2048], BF16, name="abs_v")
-        copy_v = const.tile([P, 2048], BF16, name="copy_v")
+        ones_bf = const.tile([P, 1], BF16, name="ones_bf")
+        col_sum = const.tile([P, 1], F32, name="col_sum")
         thr = const.tile([P, 1], F32, name="thr")
-        neg_thr = const.tile([P, 1], F32, name="neg_thr")
         w_sb = [const.tile([P, 4 * K_OUT], BF16, name="w_sb%d" % g) for g in range(2)]
+        a_sb = [const.tile([P, 4 * K_OUT], BF16, name="a_sb%d" % g) for g in range(2)]
+        s_sb = {(g, h): const.tile([P, 4 * HALF], BF16, name="s_sb%d%d" % (g, h)) for g in range(2) for h in range(2)}
         q_codes = const.tile([P, 2 * K_OUT], U32, name="q_codes", align_bytes=256)
         q_scales = const.tile([P, 2 * K_OUT], U8, name="q_scales", align_bytes=256)
 
         nc.vector.memset(warm[:], 0.0)
-        nc.scalar.activation(out=warm[:], in_=warm[:], func=ACTF.Abs)
+        nc.scalar.activation(out=warm[:], in_=warm[:], func=ACTF.Sign)
+        nc.vector.memset(ones_bf[:], 1.0)
         nc.vector.memset(ones[:], 1.0)
         make_identity(nc, ident[:])
 
@@ -69,13 +70,14 @@ def tile_bitlinear_t_kernel(tc, x, weight, bias, grad_out, out):
         g_t = {}
         g_codes = {}
         g_scales = {}
-        below = {}
         q_bf = {}
 
-        def load_weight(k):
+        def load_weight(t, rows):
+            g, base = t // 4, t % 4
+            k = t // 2
             nc.sync.dma_start(
-                out=w_sb[k // 2][:, (k % 2) * 2048 : (k % 2 + 1) * 2048],
-                in_=weight[256 * k : 256 * (k + 1), :].rearrange("(p e) c -> p (e c)", e=2),
+                out=w_sb[g][:, base * K_OUT : (base + rows) * K_OUT].rearrange("p (e c) -> p e c", e=rows),
+                in_=weight[256 * k : 256 * (k + 1), :].rearrange("(p e) c -> p e c", e=2)[:, t % 2 : t % 2 + rows, :],
             )
 
         def load_tokens(s):
@@ -85,64 +87,58 @@ def tile_bitlinear_t_kernel(tc, x, weight, bias, grad_out, out):
                 in_=grad_out[512 * s : 512 * (s + 1), :].rearrange("(p j) n -> p (j n)", j=4),
             )
 
-        def abs_sum(k):
-            base = (k % 2) * 2048
-            nc.scalar.activation(
-                out=abs_s[:, 0:SCALAR_SUM_COLS],
-                in_=w_sb[k // 2][:, base : base + SCALAR_SUM_COLS],
-                func=ACTF.Abs,
-                accum_out=sum_s[:, k : k + 1],
-            )
-            cols = 2048 - SCALAR_SUM_COLS
+        def take_abs(t, rows):
+            cols = slice((t % 4) * K_OUT, (t % 4 + rows) * K_OUT)
             nc.vector.tensor_scalar(
-                out=abs_v[:, 0:cols].bitcast(I32),
-                in0=w_sb[k // 2][:, base + SCALAR_SUM_COLS : base + 2048].bitcast(I32),
-                scalar1=0x7FFF7FFF, scalar2=None, op0=ALU.bitwise_and,
+                out=a_sb[t // 4][:, cols].bitcast(I32), in0=w_sb[t // 4][:, cols].bitcast(I32),
+                scalar1=ABS_BITS, scalar2=None, op0=ALU.bitwise_and,
             )
-            nc.vector.tensor_scalar(
-                out=copy_v[:, 0:cols], in0=abs_v[:, 0:cols], scalar1=1.0, scalar2=None,
-                op0=ALU.mult, op1=ALU.add, accum_out=sum_v[:, k : k + 1],
-            )
+
+        def add_up(t, rows):
+            for c in range((t % 4) * K_OUT, (t % 4 + rows) * K_OUT, P):
+                nc.tensor.matmul(
+                    out=total[:, 0:1], lhsT=a_sb[t // 4][:, c : c + P], rhs=ones_bf[:],
+                    start=(t == 0 and c == 0), stop=(t // 4 == 1 and c == 4 * K_OUT - P),
+                )
+
+        def sign_of(k, h):
+            g, u = k // 2, k % 2
+            dst = s_sb[(g, h)][:, u * 2 * HALF : (u + 1) * 2 * HALF]
+            src = w_sb[g][:, u * 2048 : (u + 1) * 2048]
+            if h == 0:
+                nc.scalar.activation(
+                    out=dst.rearrange("p (e c) -> p e c", e=2),
+                    in_=src.rearrange("p (e c) -> p e c", e=2)[:, :, 0:HALF],
+                    func=ACTF.Sign,
+                )
+            else:
+                nc.vector.tensor_scalar(
+                    out=dst.bitcast(I32).rearrange("p (e c) -> p e c", e=2),
+                    in0=src.bitcast(I32).rearrange("p (e c) -> p e c", e=2)[:, :, HALF // 2 : HALF],
+                    scalar1=SIGN_BITS, scalar2=ONE_BITS, op0=ALU.bitwise_and, op1=ALU.bitwise_or,
+                )
 
         def threshold():
-            total = psum.tile([P, HALF], F32, name="total", tag="bank")
-            for k in range(4):
-                nc.tensor.matmul(out=total[:, 0:1], lhsT=ones[:], rhs=sum_v[:, k : k + 1], start=(k == 0), stop=False)
-                nc.tensor.matmul(out=total[:, 0:1], lhsT=ones[:], rhs=sum_s[:, k : k + 1], start=False, stop=(k == 3))
-            per_element = THRESHOLD / (N_CON * K_OUT)
+            nc.vector.tensor_copy(out=col_sum[:], in_=total[:, 0:1])
+            grand = psum.tile([P, HALF], F32, name="grand", tag="bank")
+            nc.tensor.matmul(out=grand[:, 0:1], lhsT=ones[:], rhs=col_sum[:], start=True, stop=True)
             nc.vector.tensor_scalar(
-                out=neg_thr[:], in0=total[:, 0:1], scalar1=-per_element, scalar2=-THRESHOLD * EPS,
-                op0=ALU.mult, op1=ALU.min,
-            )
-            nc.vector.tensor_scalar(
-                out=thr[:], in0=total[:, 0:1], scalar1=per_element, scalar2=THRESHOLD * EPS,
+                out=thr[:], in0=grand[:, 0:1], scalar1=THRESHOLD / (N_CON * K_OUT), scalar2=THRESHOLD * EPS,
                 op0=ALU.mult, op1=ALU.max,
-            )
-
-        def w_quarter(g, h):
-            return w_sb[g][:].rearrange("p (t c) -> p t c", t=4)[:, :, h * HALF : (h + 1) * HALF]
-
-        def mark_below(g, h):
-            below[(g, h)] = qw_pool.tile([P, 4 * HALF], BF16, name="below%d%d" % (g, h), tag="below")
-            nc.vector.tensor_scalar(
-                out=below[(g, h)][:].rearrange("p (t c) -> p t c", t=4),
-                in0=w_quarter(g, h), scalar1=neg_thr[:, 0:1], scalar2=None, op0=ALU.is_lt,
             )
 
         def ternarise(g, h):
             q_bf[(g, h)] = qw_pool.tile([P, 4 * HALF], BF16, name="q_bf%d%d" % (g, h), tag="q_bf", align_bytes=64)
             nc.vector.scalar_tensor_tensor(
                 out=q_bf[(g, h)][:].rearrange("p (c t) -> p c t", t=4),
-                in0=w_quarter(g, h).rearrange("p t c -> p c t"),
+                in0=a_sb[g][:].rearrange("p (t c) -> p c t", t=4)[:, h * HALF : (h + 1) * HALF, :],
                 scalar=thr[:, 0:1],
-                in1=below[(g, h)][:].rearrange("p (t c) -> p c t", t=4),
+                in1=s_sb[(g, h)][:].rearrange("p (t c) -> p c t", t=4),
                 op0=ALU.is_gt,
-                op1=ALU.subtract,
+                op1=ALU.mult,
             )
 
         def build_half_of_q(h):
-            mark_below(0, h)
-            mark_below(1, h)
             ternarise(0, h)
             ternarise(1, h)
             quantise_q(0, h)
@@ -230,12 +226,30 @@ def tile_bitlinear_t_kernel(tc, x, weight, bias, grad_out, out):
         def one_tile(s, j, scalar_banks):
             products(s, [(j, 0), (j, 1)], group_rows(s)[:, j : j + 1, :], scalar_banks)
 
-        for k in range(4):
-            load_weight(k)
+        pieces = [(0, 2), (2, 2), (4, 2), (6, 1), (7, 1)]
+        for t, rows in pieces:
+            load_weight(t, rows)
         for s in range(G_RESIDENT):
             load_tokens(s)
-        for k in range(4):
-            abs_sum(k)
+        total = psum.tile([P, HALF], F32, name="total", tag="bank")
+        take_abs(0, 2)
+        add_up(0, 2)
+        sign_of(0, 0)
+        sign_of(0, 1)
+        take_abs(2, 2)
+        add_up(2, 2)
+        sign_of(1, 0)
+        sign_of(1, 1)
+        take_abs(4, 2)
+        add_up(4, 2)
+        sign_of(2, 0)
+        take_abs(6, 1)
+        add_up(6, 1)
+        take_abs(7, 1)
+        add_up(7, 1)
+        sign_of(3, 0)
+        sign_of(2, 1)
+        sign_of(3, 1)
         threshold()
 
         transposes(0, True)

@@ -27,6 +27,8 @@ GROUPS = TOKENS // 512
 HALF = 512
 G_RESIDENT = 6
 
+SUM_COLS = 256
+
 ABS_BITS = 0x7FFF7FFF
 SIGN_BITS = -0x7FFF8000
 ONE_BITS = 0x3F803F80
@@ -41,28 +43,30 @@ def tile_bitlinear_t_kernel(tc, x, weight, bias, grad_out, out):
         const = ctx.enter_context(tc.tile_pool(name="const", bufs=1))
         g_pool = ctx.enter_context(tc.tile_pool(name="g_pool", bufs=G_RESIDENT))
         gg_pool = ctx.enter_context(tc.tile_pool(name="gg_pool", bufs=3))
-        gc_pool = ctx.enter_context(tc.tile_pool(name="gc_pool", bufs=6))
+        gc_pool = ctx.enter_context(tc.tile_pool(name="gc_pool", bufs=GROUPS))
         qw_pool = ctx.enter_context(tc.tile_pool(name="qw_pool", bufs=2))
-        st_pool = ctx.enter_context(tc.tile_pool(name="st_pool", bufs=4))
-        s1_pool = ctx.enter_context(tc.tile_pool(name="s1_pool", bufs=6))
-        psum = ctx.enter_context(tc.psum_pool(name="psum", bufs=8))
+        st_pool = ctx.enter_context(tc.tile_pool(name="st_pool", bufs=7))
+        psum = ctx.enter_context(tc.psum_pool(name="psum", bufs=1))
         ctx.enter_context(tc.manual_schedule())
 
         ident = const.tile([P, P], F32, name="ident")
-        ones = const.tile([P, P], F32, name="ones")
+        ones = const.tile([P, P], BF16, name="ones")
         warm = const.tile([P, 1], F32, name="warm")
-        ones_bf = const.tile([P, 1], BF16, name="ones_bf")
-        col_sum = const.tile([P, 1], F32, name="col_sum")
+        busy = const.tile([P, HALF], BF16, name="busy")
+        parts_sum = const.tile([P, SUM_COLS], F32, name="parts_sum")
+        mean_t = const.tile([P, 1], F32, name="mean_t")
         thr = const.tile([P, 1], F32, name="thr")
-        w_sb = [const.tile([P, 4 * K_OUT], BF16, name="w_sb%d" % g) for g in range(2)]
+        w_sb = [st_pool.tile([P, 4 * K_OUT], BF16, name="w_sb%d" % g, tag="staged") for g in range(2)]
         a_sb = [const.tile([P, 4 * K_OUT], BF16, name="a_sb%d" % g) for g in range(2)]
-        s_sb = {(g, h): const.tile([P, 4 * HALF], BF16, name="s_sb%d%d" % (g, h)) for g in range(2) for h in range(2)}
+        a_i = {g: const.tile([P, 4 * HALF], BF16, name="a_i%d" % g) for g in range(2)}
+        s_i = {g: const.tile([P, 4 * HALF], BF16, name="s_i%d" % g) for g in range(2)}
+        s_sb = {g: const.tile([P, 4 * HALF], BF16, name="s_sb%d" % g) for g in range(2)}
         q_codes = const.tile([P, 2 * K_OUT], U32, name="q_codes", align_bytes=256)
         q_scales = const.tile([P, 2 * K_OUT], U8, name="q_scales", align_bytes=256)
 
         nc.vector.memset(warm[:], 0.0)
         nc.scalar.activation(out=warm[:], in_=warm[:], func=ACTF.Sign)
-        nc.vector.memset(ones_bf[:], 1.0)
+        nc.vector.memset(busy[:], 1.0)
         nc.vector.memset(ones[:], 1.0)
         make_identity(nc, ident[:])
 
@@ -70,14 +74,23 @@ def tile_bitlinear_t_kernel(tc, x, weight, bias, grad_out, out):
         g_t = {}
         g_codes = {}
         g_scales = {}
+        row_tile = {}
         q_bf = {}
 
+        bank_of = {"next": 0}
+
+        def bank(place=None):
+            if place is None:
+                place = bank_of["next"] % 8
+                bank_of["next"] += 1
+            tile = psum.tile([P, HALF], F32, name="bank%d" % place, tag="bank%d" % place)
+            return tile
+
         def load_weight(t, rows):
-            g, base = t // 4, t % 4
-            k = t // 2
+            k, base = t // 2, t % 2
             nc.sync.dma_start(
-                out=w_sb[g][:, base * K_OUT : (base + rows) * K_OUT].rearrange("p (e c) -> p e c", e=rows),
-                in_=weight[256 * k : 256 * (k + 1), :].rearrange("(p e) c -> p e c", e=2)[:, t % 2 : t % 2 + rows, :],
+                out=w_sb[t // 4][:, (t % 4) * K_OUT : (t % 4 + rows) * K_OUT].rearrange("p (e c) -> p e c", e=rows),
+                in_=weight[256 * k : 256 * (k + 1), :].rearrange("(p e) c -> p e c", e=2)[:, base : base + rows, :],
             )
 
         def load_tokens(s):
@@ -95,54 +108,66 @@ def tile_bitlinear_t_kernel(tc, x, weight, bias, grad_out, out):
             )
 
         def add_up(t, rows):
-            for c in range((t % 4) * K_OUT, (t % 4 + rows) * K_OUT, P):
+            for c in range((t % 4) * K_OUT, (t % 4 + rows) * K_OUT, SUM_COLS):
                 nc.tensor.matmul(
-                    out=total[:, 0:1], lhsT=a_sb[t // 4][:, c : c + P], rhs=ones_bf[:],
-                    start=(t == 0 and c == 0), stop=(t // 4 == 1 and c == 4 * K_OUT - P),
+                    out=total[:, 0:SUM_COLS], lhsT=ones[:], rhs=a_sb[t // 4][:, c : c + SUM_COLS],
+                    start=(t == 0 and c == 0), stop=(t // 4 == 1 and c == 4 * K_OUT - SUM_COLS),
                 )
 
-        def sign_of(k, h):
-            g, u = k // 2, k % 2
-            dst = s_sb[(g, h)][:, u * 2 * HALF : (u + 1) * 2 * HALF]
-            src = w_sb[g][:, u * 2048 : (u + 1) * 2048]
-            if h == 0:
-                nc.scalar.activation(
-                    out=dst.rearrange("p (e c) -> p e c", e=2),
-                    in_=src.rearrange("p (e c) -> p e c", e=2)[:, :, 0:HALF],
-                    func=ACTF.Sign,
-                )
-            else:
-                nc.vector.tensor_scalar(
-                    out=dst.bitcast(I32).rearrange("p (e c) -> p e c", e=2),
-                    in0=src.bitcast(I32).rearrange("p (e c) -> p e c", e=2)[:, :, HALF // 2 : HALF],
-                    scalar1=SIGN_BITS, scalar2=ONE_BITS, op0=ALU.bitwise_and, op1=ALU.bitwise_or,
-                )
+        def keep_busy(n, place):
+            idle = bank(place)
+            for i in range(n):
+                nc.tensor.matmul(out=idle[:], lhsT=ones[:], rhs=busy[:], start=True, stop=True)
 
-        def threshold():
-            nc.vector.tensor_copy(out=col_sum[:], in_=total[:, 0:1])
-            grand = psum.tile([P, HALF], F32, name="grand", tag="bank")
-            nc.tensor.matmul(out=grand[:, 0:1], lhsT=ones[:], rhs=col_sum[:], start=True, stop=True)
+        def quarter(tile, h):
+            return tile[:].rearrange("p (t c) -> p c t", t=4)[:, h * HALF : (h + 1) * HALF, :]
+
+        def by_word(tile):
+            return tile[:].rearrange("p (c t) -> p c t", t=4)
+
+        def sign_bits(dst, src):
             nc.vector.tensor_scalar(
-                out=thr[:], in0=grand[:, 0:1], scalar1=THRESHOLD / (N_CON * K_OUT), scalar2=THRESHOLD * EPS,
-                op0=ALU.mult, op1=ALU.max,
+                out=dst, in0=src, scalar1=SIGN_BITS, scalar2=ONE_BITS, op0=ALU.bitwise_and, op1=ALU.bitwise_or,
             )
 
-        def ternarise(g, h):
+        def sign_half_1(k):
+            g, u = k // 2, k % 2
+            sign_bits(
+                s_sb[g][:, u * 2 * HALF : (u + 1) * 2 * HALF].bitcast(I32).rearrange("p (e c) -> p e c", e=2),
+                w_sb[g][:, u * 2048 : (u + 1) * 2048].bitcast(I32).rearrange("p (e c) -> p e c", e=2)[:, :, HALF // 2 : HALF],
+            )
+
+        def threshold():
+            nc.vector.tensor_scalar(
+                out=parts_sum[:], in0=total[:, 0:SUM_COLS], scalar1=THRESHOLD / (N_CON * K_OUT), scalar2=None,
+                op0=ALU.mult, op1=ALU.add, accum_out=mean_t[:],
+            )
+            order_abs(1)
+            nc.vector.tensor_scalar(out=thr[:], in0=mean_t[:], scalar1=THRESHOLD * EPS, scalar2=None, op0=ALU.max)
+
+        def q_tile(g, h):
             q_bf[(g, h)] = qw_pool.tile([P, 4 * HALF], BF16, name="q_bf%d%d" % (g, h), tag="q_bf", align_bytes=64)
+            return q_bf[(g, h)]
+
+        def order_abs(part):
+            cols = slice(part * HALF // 2, (part + 1) * HALF // 2)
+            nc.vector.tensor_copy(out=by_word(a_i[1])[:, cols, :], in_=quarter(a_sb[1], 0)[:, cols, :])
+
+        def exceeds(g):
+            nc.vector.tensor_scalar(out=a_i[g][:], in0=a_i[g][:], scalar1=thr[:, 0:1], scalar2=None, op0=ALU.is_gt)
+
+        def ternarise_half_0(g):
+            nc.vector.tensor_tensor(out=q_tile(g, 0)[:], in0=a_i[g][:], in1=s_i[g][:], op=ALU.mult)
+
+        def ternarise_half_1(g):
             nc.vector.scalar_tensor_tensor(
-                out=q_bf[(g, h)][:].rearrange("p (c t) -> p c t", t=4),
-                in0=a_sb[g][:].rearrange("p (t c) -> p c t", t=4)[:, h * HALF : (h + 1) * HALF, :],
+                out=by_word(q_tile(g, 1)),
+                in0=quarter(a_sb[g], 1),
                 scalar=thr[:, 0:1],
-                in1=s_sb[(g, h)][:].rearrange("p (t c) -> p c t", t=4),
+                in1=s_sb[g][:].rearrange("p (t c) -> p c t", t=4),
                 op0=ALU.is_gt,
                 op1=ALU.mult,
             )
-
-        def build_half_of_q(h):
-            ternarise(0, h)
-            ternarise(1, h)
-            quantise_q(0, h)
-            quantise_q(1, h)
 
         def q_cols(g, h):
             return slice(g * K_OUT + h * HALF, g * K_OUT + (h + 1) * HALF)
@@ -154,28 +179,28 @@ def tile_bitlinear_t_kernel(tc, x, weight, bias, grad_out, out):
                 in_=q_bf[(g, h)][:],
             )
 
-        def copy_out(on_scalar, dst, src):
-            if on_scalar:
+        def copy_out(engine, dst, src):
+            if engine == "S":
                 nc.scalar.copy(out=dst, in_=src)
             else:
                 nc.vector.tensor_copy(out=dst, in_=src)
 
-        def transposes(s, on_scalar):
+        def transposes(s, engines, first=None):
             g_t[s] = gg_pool.tile([P, 4 * N_CON], BF16, name="g_t%d" % s, tag="g_t", align_bytes=64)
             words = g_sb[s][:].bitcast(F32)
             banks = []
             for j in range(4):
-                bank = psum.tile([P, HALF], F32, name="tp%d_%d" % (s, j), tag="bank")
+                tp = bank(None if first is None else first + j)
                 for k in range(4):
                     nc.tensor.transpose(
-                        out=bank[:, k * 128 : (k + 1) * 128],
+                        out=tp[:, k * 128 : (k + 1) * 128],
                         in_=words[:, j * 512 + k * 128 : j * 512 + (k + 1) * 128],
                         identity=ident[:],
                     )
-                banks.append(bank)
+                banks.append(tp)
             for j in range(4):
                 copy_out(
-                    on_scalar,
+                    engines[j],
                     g_t[s][:].bitcast(F32)[:, j * 512 : (j + 1) * 512].rearrange("p (g m u) -> p g m u", g=2, u=2),
                     banks[j][:].rearrange("p (g u m) -> p g m u", g=2, u=2),
                 )
@@ -186,105 +211,151 @@ def tile_bitlinear_t_kernel(tc, x, weight, bias, grad_out, out):
         def scale_cols(j, g):
             return slice(SCALE_SLOT * (2 * j + g), SCALE_SLOT * (2 * j + g) + 128)
 
-        def quantise_tokens(s):
+        def code_tiles(s):
             g_codes[s] = gc_pool.tile([P, CODE_PAD + 1024], U32, name="g_codes%d" % s, tag="g_codes", align_bytes=256)
             g_scales[s] = gc_pool.tile([P, 8 * SCALE_SLOT], U8, name="g_scales%d" % s, tag="g_scales", align_bytes=256)
-            for j in range(4):
-                for g in range(2):
+
+        def quantise_tokens(s, passes, tiles=range(4)):
+            for j in tiles:
+                for g in passes:
                     nc.vector.quantize_mx(
                         out=g_codes[s][:, code_cols(j, g)].bitcast(E5M2X4),
                         scales=g_scales[s][:, scale_cols(j, g)],
                         in_=g_t[s][:, 512 * (2 * j + g) : 512 * (2 * j + g + 1)],
                     )
 
-        def products(s, parts, dram, scalar_banks):
-            if len(parts) == 4:
-                staged = st_pool.tile([P, 4 * HALF], F32, name="staged4", tag="staged4")
-            else:
-                staged = s1_pool.tile([P, 2 * HALF], F32, name="staged2", tag="staged2")
-            for i, (j, h) in enumerate(parts):
-                acc = psum.tile([P, HALF], F32, name="acc", tag="bank")
-                for g in range(2):
-                    nc.tensor.matmul_mx(
-                        out=acc[:],
-                        lhsT=g_codes[s][:, code_cols(j, g)].bitcast(E5M2X4),
-                        lhsT_scale=g_scales[s][:, scale_cols(j, g)],
-                        rhs=q_codes[:, q_cols(g, h)].bitcast(E4M3X4),
-                        rhs_scale=q_scales[:, q_cols(g, h)],
-                        start=(g == 0),
-                        stop=(g == 1),
-                    )
-                copy_out(i < scalar_banks, staged[:, i * HALF : (i + 1) * HALF], acc[:])
-            nc.sync.dma_start(out=dram, in_=staged[:].rearrange("p (r c) -> p r c", r=dram.shape[1]))
+        def mx_pass(s, j, h, g, acc):
+            nc.tensor.matmul_mx(
+                out=acc[:],
+                lhsT=g_codes[s][:, code_cols(j, g)].bitcast(E5M2X4),
+                lhsT_scale=g_scales[s][:, scale_cols(j, g)],
+                rhs=q_codes[:, q_cols(g, h)].bitcast(E4M3X4),
+                rhs_scale=q_scales[:, q_cols(g, h)],
+                start=(g == 0),
+                stop=(g == 1),
+            )
+
+        def product(s, j, h, place=None):
+            acc = bank(place)
+            for g in range(2):
+                mx_pass(s, j, h, g, acc)
+            return acc
 
         def group_rows(s):
             return out[512 * s : 512 * (s + 1), :].rearrange("(p j) c -> p j c", j=4)
 
-        def half_of_group(s, h, scalar_banks):
-            products(s, [(j, h) for j in range(4)], group_rows(s)[:, :, h * HALF : (h + 1) * HALF], scalar_banks)
+        def half_products(s, h, accs, engines):
+            staged = st_pool.tile([P, 4 * HALF], F32, name="staged_h", tag="staged")
+            for j in range(4):
+                copy_out(engines[j], staged[:, j * HALF : (j + 1) * HALF], accs[j][:])
+                if j % 2 == 1:
+                    nc.sync.dma_start(
+                        out=group_rows(s)[:, j - 1 : j + 1, h * HALF : (h + 1) * HALF],
+                        in_=staged[:, (j - 1) * HALF : (j + 1) * HALF].rearrange("p (r c) -> p r c", r=2),
+                    )
 
-        def one_tile(s, j, scalar_banks):
-            products(s, [(j, 0), (j, 1)], group_rows(s)[:, j : j + 1, :], scalar_banks)
+        def half_of_group(s, h, engines, first=None):
+            half_products(s, h, [product(s, j, h, None if first is None else first + j) for j in range(4)], engines)
+
+        def fill(s, j, parts, engines):
+            if (s, j) not in row_tile:
+                row_tile[(s, j)] = st_pool.tile([P, 2 * K_OUT], F32, name="staged_w", tag="staged")
+            for i, (jj, h) in enumerate(parts):
+                c = (jj - j) * K_OUT + h * HALF
+                copy_out(engines[i], row_tile[(s, j)][:, c : c + HALF], product(s, jj, h)[:])
+
+        def store_rows(s, j, first, tiles):
+            c = (first - j) * K_OUT
+            nc.sync.dma_start(
+                out=group_rows(s)[:, first : first + tiles, :],
+                in_=row_tile[(s, j)][:, c : c + tiles * K_OUT].rearrange("p (r c) -> p r c", r=tiles),
+            )
+
+        def two_tiles(s, j, engines):
+            fill(s, j, [(j, 0), (j, 1), (j + 1, 0), (j + 1, 1)], engines)
+            store_rows(s, j, j, 2)
 
         pieces = [(0, 2), (2, 2), (4, 2), (6, 1), (7, 1)]
         for t, rows in pieces:
             load_weight(t, rows)
         for s in range(G_RESIDENT):
             load_tokens(s)
-        total = psum.tile([P, HALF], F32, name="total", tag="bank")
+        keep_busy(6, 4)
+        total = bank(7)
         take_abs(0, 2)
         add_up(0, 2)
-        sign_of(0, 0)
-        sign_of(0, 1)
         take_abs(2, 2)
         add_up(2, 2)
-        sign_of(1, 0)
-        sign_of(1, 1)
+        nc.scalar.copy(out=by_word(a_i[0]), in_=quarter(w_sb[0], 0))
+        sign_half_1(0)
         take_abs(4, 2)
         add_up(4, 2)
-        sign_of(2, 0)
         take_abs(6, 1)
         add_up(6, 1)
         take_abs(7, 1)
         add_up(7, 1)
-        sign_of(3, 0)
-        sign_of(2, 1)
-        sign_of(3, 1)
+        nc.scalar.activation(out=by_word(s_i[1]), in_=quarter(w_sb[1], 0), func=ACTF.Sign)
+        sign_bits(s_i[0][:].bitcast(I32), a_i[0][:].bitcast(I32))
+        nc.vector.tensor_scalar(
+            out=a_i[0][:].bitcast(I32), in0=a_i[0][:].bitcast(I32), scalar1=ABS_BITS, scalar2=None, op0=ALU.bitwise_and,
+        )
+        order_abs(0)
         threshold()
 
-        transposes(0, True)
+        keep_busy(2, 4)
+        for s in range(GROUPS):
+            code_tiles(s)
+        exceeds(0)
+        transposes(0, "SSSS", 0)
+        keep_busy(2, 4)
         load_tokens(6)
-        transposes(1, True)
+        sign_half_1(1)
+        ternarise_half_0(0)
+        exceeds(1)
+        transposes(1, "SSSS", 4)
         load_tokens(7)
-        build_half_of_q(0)
-        transposes(2, True)
-        quantise_tokens(0)
-        transposes(3, True)
-        quantise_tokens(1)
-
-        half_of_group(0, 0, 4)
-        quantise_tokens(2)
-        half_of_group(1, 0, 4)
-        transposes(4, True)
-        build_half_of_q(1)
-        half_of_group(2, 0, 3)
-        transposes(5, False)
-        quantise_tokens(3)
-
-        half_of_group(0, 1, 3)
-        half_of_group(1, 1, 3)
-        transposes(6, False)
-        quantise_tokens(4)
-        half_of_group(2, 1, 3)
-        one_tile(3, 0, 2)
-        one_tile(3, 1, 1)
-        transposes(7, False)
-        quantise_tokens(5)
-        one_tile(3, 2, 2)
-        one_tile(3, 3, 1)
-
+        quantise_tokens(0, (0,), (0, 1))
+        quantise_q(0, 0)
+        quantise_tokens(0, (0,), (2, 3))
+        accs = [bank(j) for j in range(4)]
+        for j in range(4):
+            mx_pass(0, j, 0, 0, accs[j])
+        transposes(2, "SSSS", 4)
+        ternarise_half_0(1)
+        quantise_tokens(0, (1,))
+        quantise_q(1, 0)
+        for j in range(4):
+            mx_pass(0, j, 0, 1, accs[j])
+        quantise_tokens(1, (0, 1))
+        half_products(0, 0, accs, "SSSS")
+        half_of_group(1, 0, "SSSS", 4)
+        sign_half_1(2)
+        sign_half_1(3)
+        transposes(3, "SSSS", 0)
+        quantise_tokens(2, (0, 1))
+        ternarise_half_1(0)
+        half_of_group(2, 0, "SSSS", 4)
+        transposes(4, "SSSS", 0)
+        ternarise_half_1(1)
+        quantise_tokens(3, (0, 1))
+        half_of_group(3, 0, "SSSS", 4)
+        quantise_q(0, 1)
+        quantise_q(1, 1)
+        half_of_group(0, 1, "SVSV")
+        half_of_group(1, 1, "SVSV")
+        half_of_group(2, 1, "SVSV")
+        half_of_group(3, 1, "SVSV")
+        quantise_tokens(4, (0, 1))
+        transposes(5, "SVSV")
         for s in range(4, GROUPS):
-            for j in range(4):
-                one_tile(s, j, 1)
-                if j == 1 and s + 2 < GROUPS:
-                    quantise_tokens(s + 2)
+            if s + 1 < GROUPS:
+                quantise_tokens(s + 1, (0, 1))
+            two_tiles(s, 0, "SVSV")
+            if s + 2 < GROUPS:
+                transposes(s + 2, "SVSV")
+            if s < 7:
+                two_tiles(s, 2, "SVSV")
+            else:
+                for j in (2, 3):
+                    fill(s, 2, [(j, 0), (j, 1)], "SV")
+                    store_rows(s, 2, j, 1)

@@ -58,7 +58,7 @@ def tile_bitlinear_t_kernel(tc, x, weight, bias, grad_out, out):
         thr = const.tile([P, 1], F32, name="thr")
         w_sb = [st_pool.tile([P, 4 * K_OUT], BF16, name="w_sb%d" % g, tag="staged") for g in range(2)]
         a_sb = [const.tile([P, 4 * K_OUT], BF16, name="a_sb%d" % g) for g in range(2)]
-        a_i = {g: const.tile([P, 4 * HALF], BF16, name="a_i%d" % g) for g in range(2)}
+        a_i = const.tile([P, 4 * HALF], BF16, name="a_i")
         s_i = {g: const.tile([P, 4 * HALF], BF16, name="s_i%d" % g) for g in range(2)}
         s_sb = {g: const.tile([P, 4 * HALF], BF16, name="s_sb%d" % g) for g in range(2)}
         q_codes = const.tile([P, 2 * K_OUT], U32, name="q_codes", align_bytes=256)
@@ -142,29 +142,25 @@ def tile_bitlinear_t_kernel(tc, x, weight, bias, grad_out, out):
                 out=parts_sum[:], in0=total[:, 0:SUM_COLS], scalar1=THRESHOLD / (N_CON * K_OUT), scalar2=None,
                 op0=ALU.mult, op1=ALU.add, accum_out=mean_t[:],
             )
-            order_abs(1)
+            sign_half_1(2)
             nc.vector.tensor_scalar(out=thr[:], in0=mean_t[:], scalar1=THRESHOLD * EPS, scalar2=None, op0=ALU.max)
 
         def q_tile(g, h):
             q_bf[(g, h)] = qw_pool.tile([P, 4 * HALF], BF16, name="q_bf%d%d" % (g, h), tag="q_bf", align_bytes=64)
             return q_bf[(g, h)]
 
-        def order_abs(part):
-            cols = slice(part * HALF // 2, (part + 1) * HALF // 2)
-            nc.vector.tensor_copy(out=by_word(a_i[1])[:, cols, :], in_=quarter(a_sb[1], 0)[:, cols, :])
+        def exceeds():
+            nc.vector.tensor_scalar(out=a_i[:], in0=a_i[:], scalar1=thr[:, 0:1], scalar2=None, op0=ALU.is_gt)
 
-        def exceeds(g):
-            nc.vector.tensor_scalar(out=a_i[g][:], in0=a_i[g][:], scalar1=thr[:, 0:1], scalar2=None, op0=ALU.is_gt)
+        def ternarise_00():
+            nc.vector.tensor_tensor(out=q_tile(0, 0)[:], in0=a_i[:], in1=s_i[0][:], op=ALU.mult)
 
-        def ternarise_half_0(g):
-            nc.vector.tensor_tensor(out=q_tile(g, 0)[:], in0=a_i[g][:], in1=s_i[g][:], op=ALU.mult)
-
-        def ternarise_half_1(g):
+        def ternarise(g, h):
             nc.vector.scalar_tensor_tensor(
-                out=by_word(q_tile(g, 1)),
-                in0=quarter(a_sb[g], 1),
+                out=by_word(q_tile(g, h)),
+                in0=quarter(a_sb[g], h),
                 scalar=thr[:, 0:1],
-                in1=s_sb[g][:].rearrange("p (t c) -> p c t", t=4),
+                in1=by_word(s_i[g]) if h == 0 else s_sb[g][:].rearrange("p (t c) -> p c t", t=4),
                 op0=ALU.is_gt,
                 op1=ALU.mult,
             )
@@ -257,12 +253,12 @@ def tile_bitlinear_t_kernel(tc, x, weight, bias, grad_out, out):
         def half_of_group(s, h, engines, first=None):
             half_products(s, h, [product(s, j, h, None if first is None else first + j) for j in range(4)], engines)
 
-        def fill(s, j, parts, engines):
+        def fill(s, j, parts, engines, first=None):
             if (s, j) not in row_tile:
                 row_tile[(s, j)] = st_pool.tile([P, 2 * K_OUT], F32, name="staged_w", tag="staged")
             for i, (jj, h) in enumerate(parts):
                 c = (jj - j) * K_OUT + h * HALF
-                copy_out(engines[i], row_tile[(s, j)][:, c : c + HALF], product(s, jj, h)[:])
+                copy_out(engines[i], row_tile[(s, j)][:, c : c + HALF], product(s, jj, h, None if first is None else first + i)[:])
 
         def store_rows(s, j, first, tiles):
             c = (first - j) * K_OUT
@@ -282,38 +278,39 @@ def tile_bitlinear_t_kernel(tc, x, weight, bias, grad_out, out):
             load_tokens(s)
         keep_busy(6, 4)
         total = bank(7)
-        take_abs(0, 2)
-        add_up(0, 2)
-        take_abs(2, 2)
-        add_up(2, 2)
-        nc.scalar.copy(out=by_word(a_i[0]), in_=quarter(w_sb[0], 0))
+        for t in range(2):
+            take_abs(t, 1)
+            add_up(t, 1)
+        for t in range(2, 4):
+            take_abs(t, 1)
+            add_up(t, 1)
+        nc.scalar.copy(out=by_word(a_i), in_=quarter(w_sb[0], 0))
         sign_half_1(0)
-        take_abs(4, 2)
-        add_up(4, 2)
+        for t in range(4, 6):
+            take_abs(t, 1)
+            add_up(t, 1)
         take_abs(6, 1)
         add_up(6, 1)
+        sign_half_1(1)
         take_abs(7, 1)
         add_up(7, 1)
         nc.scalar.activation(out=by_word(s_i[1]), in_=quarter(w_sb[1], 0), func=ACTF.Sign)
-        sign_bits(s_i[0][:].bitcast(I32), a_i[0][:].bitcast(I32))
+        sign_bits(s_i[0][:].bitcast(I32), a_i[:].bitcast(I32))
         nc.vector.tensor_scalar(
-            out=a_i[0][:].bitcast(I32), in0=a_i[0][:].bitcast(I32), scalar1=ABS_BITS, scalar2=None, op0=ALU.bitwise_and,
+            out=a_i[:].bitcast(I32), in0=a_i[:].bitcast(I32), scalar1=ABS_BITS, scalar2=None, op0=ALU.bitwise_and,
         )
-        order_abs(0)
         threshold()
 
         keep_busy(2, 4)
         for s in range(GROUPS):
             code_tiles(s)
-        exceeds(0)
+        exceeds()
         transposes(0, "SSSS", 0)
         keep_busy(2, 4)
         load_tokens(6)
-        sign_half_1(1)
-        ternarise_half_0(0)
-        exceeds(1)
+        sign_half_1(3)
+        ternarise_00()
         transposes(1, "SSSS", 4)
-        load_tokens(7)
         quantise_tokens(0, (0,), (0, 1))
         quantise_q(0, 0)
         quantise_tokens(0, (0,), (2, 3))
@@ -321,41 +318,46 @@ def tile_bitlinear_t_kernel(tc, x, weight, bias, grad_out, out):
         for j in range(4):
             mx_pass(0, j, 0, 0, accs[j])
         transposes(2, "SSSS", 4)
-        ternarise_half_0(1)
-        quantise_tokens(0, (1,))
+        ternarise(1, 0)
+        quantise_tokens(0, (1,), (0, 1))
         quantise_q(1, 0)
+        quantise_tokens(0, (1,), (2, 3))
         for j in range(4):
             mx_pass(0, j, 0, 1, accs[j])
         quantise_tokens(1, (0, 1))
         half_products(0, 0, accs, "SSSS")
         half_of_group(1, 0, "SSSS", 4)
-        sign_half_1(2)
-        sign_half_1(3)
+        load_tokens(7)
         transposes(3, "SSSS", 0)
         quantise_tokens(2, (0, 1))
-        ternarise_half_1(0)
+        ternarise(0, 1)
         half_of_group(2, 0, "SSSS", 4)
         transposes(4, "SSSS", 0)
-        ternarise_half_1(1)
+        ternarise(1, 1)
         quantise_tokens(3, (0, 1))
-        half_of_group(3, 0, "SSSS", 4)
         quantise_q(0, 1)
         quantise_q(1, 1)
+        fill(3, 0, [(0, 0), (1, 0)], "SV", 4)
+        fill(3, 2, [(2, 0), (3, 0)], "SV", 6)
         half_of_group(0, 1, "SVSV")
+        quantise_tokens(4, (0, 1))
         half_of_group(1, 1, "SVSV")
         half_of_group(2, 1, "SVSV")
-        half_of_group(3, 1, "SVSV")
-        quantise_tokens(4, (0, 1))
+        fill(3, 0, [(0, 1), (1, 1)], "SV")
+        store_rows(3, 0, 0, 2)
+        fill(3, 2, [(2, 1), (3, 1)], "SV")
+        store_rows(3, 2, 2, 2)
         transposes(5, "SVSV")
+        transposes(6, "SVSV")
+        quantise_tokens(5, (0, 1))
         for s in range(4, GROUPS):
-            if s + 1 < GROUPS:
+            if 5 < s + 1 < GROUPS:
                 quantise_tokens(s + 1, (0, 1))
-            two_tiles(s, 0, "SVSV")
-            if s + 2 < GROUPS:
-                transposes(s + 2, "SVSV")
-            if s < 7:
-                two_tiles(s, 2, "SVSV")
-            else:
-                for j in (2, 3):
-                    fill(s, 2, [(j, 0), (j, 1)], "SV")
-                    store_rows(s, 2, j, 1)
+            for j in range(4):
+                fill(s, j - j % 2, [(j, 0), (j, 1)], "SV")
+                if s in (7,):
+                    store_rows(s, j - j % 2, j, 1)
+                elif j % 2 == 1:
+                    store_rows(s, j - 1, j - 1, 2)
+                if s == 4 and j == 3:
+                    transposes(7, "SVSV")

@@ -311,6 +311,7 @@ def tile_bitlinear_t_kernel(tc, x, weight, bias, grad_out, out):
         sign_half_1(3)
         ternarise_00()
         transposes(1, "SSSS", 4)
+        keep_busy(1, 0)
         quantise_tokens(0, (0,), (0, 1))
         quantise_q(0, 0)
         quantise_tokens(0, (0,), (2, 3))
@@ -318,6 +319,7 @@ def tile_bitlinear_t_kernel(tc, x, weight, bias, grad_out, out):
         for j in range(4):
             mx_pass(0, j, 0, 0, accs[j])
         transposes(2, "SSSS", 4)
+        keep_busy(3, 4)
         ternarise(1, 0)
         quantise_tokens(0, (1,), (0, 1))
         quantise_q(1, 0)
@@ -342,14 +344,14 @@ def tile_bitlinear_t_kernel(tc, x, weight, bias, grad_out, out):
         half_of_group(0, 1, "SVSV")
         quantise_tokens(4, (0, 1))
         half_of_group(1, 1, "SVSV")
+        transposes(5, "SVSV")
         half_of_group(2, 1, "SVSV")
+        quantise_tokens(5, (0, 1))
         fill(3, 0, [(0, 1), (1, 1)], "SV")
         store_rows(3, 0, 0, 2)
         fill(3, 2, [(2, 1), (3, 1)], "SV")
         store_rows(3, 2, 2, 2)
-        transposes(5, "SVSV")
         transposes(6, "SVSV")
-        quantise_tokens(5, (0, 1))
         for s in range(4, GROUPS):
             if 5 < s + 1 < GROUPS:
                 quantise_tokens(s + 1, (0, 1))

@@ -181,8 +181,7 @@ def tile_bitlinear_t_kernel(tc, x, weight, bias, grad_out, out):
             else:
                 nc.vector.tensor_copy(out=dst, in_=src)
 
-        def transposes(s, engines, first=None):
-            g_t[s] = gg_pool.tile([P, 4 * N_CON], BF16, name="g_t%d" % s, tag="g_t", align_bytes=64)
+        def turn(s, first=None):
             words = g_sb[s][:].bitcast(F32)
             banks = []
             for j in range(4):
@@ -194,12 +193,19 @@ def tile_bitlinear_t_kernel(tc, x, weight, bias, grad_out, out):
                         identity=ident[:],
                     )
                 banks.append(tp)
+            return banks
+
+        def lay_out(s, banks, engines):
+            g_t[s] = gg_pool.tile([P, 4 * N_CON], BF16, name="g_t%d" % s, tag="g_t", align_bytes=64)
             for j in range(4):
                 copy_out(
                     engines[j],
                     g_t[s][:].bitcast(F32)[:, j * 512 : (j + 1) * 512].rearrange("p (g m u) -> p g m u", g=2, u=2),
                     banks[j][:].rearrange("p (g u m) -> p g m u", g=2, u=2),
                 )
+
+        def transposes(s, engines, first=None):
+            lay_out(s, turn(s, first), engines)
 
         def code_cols(j, g):
             return slice(CODE_PAD + 128 * (2 * j + g), CODE_PAD + 128 * (2 * j + g + 1))
@@ -319,47 +325,72 @@ def tile_bitlinear_t_kernel(tc, x, weight, bias, grad_out, out):
         for j in range(4):
             mx_pass(0, j, 0, 0, accs[j])
         transposes(2, "SSSS", 4)
-        keep_busy(3, 4)
         ternarise(1, 0)
-        quantise_tokens(0, (1,), (0, 1))
+        quantise_tokens(1, (0,), (0, 1))
         quantise_q(1, 0)
-        quantise_tokens(0, (1,), (2, 3))
+        quantise_tokens(0, (1,))
+        early = [bank(4), bank(5)]
+        for j in range(2):
+            mx_pass(1, j, 0, 0, early[j])
         for j in range(4):
             mx_pass(0, j, 0, 1, accs[j])
-        quantise_tokens(1, (0, 1))
+        quantise_tokens(1, (1,), (0, 1))
         half_products(0, 0, accs, "SSSS")
-        half_of_group(1, 0, "SSSS", 4)
+        for j in range(2):
+            mx_pass(1, j, 0, 1, early[j])
+        quantise_tokens(1, (0, 1), (2, 3))
+        half_products(1, 0, early + [product(1, 2, 0, 6), product(1, 3, 0, 7)], "SSSS")
         load_tokens(7)
         transposes(3, "SSSS", 0)
         quantise_tokens(2, (0, 1))
         ternarise(0, 1)
         half_of_group(2, 0, "SSSS", 4)
-        transposes(4, "SSSS", 0)
+        turned = turn(4, 0)
         ternarise(1, 1)
         quantise_tokens(3, (0, 1))
         quantise_q(0, 1)
         quantise_q(1, 1)
+        lay_out(4, turned, "VVVV")
         fill(3, 0, [(0, 0), (1, 0)], "SV", 4)
         fill(3, 2, [(2, 0), (3, 0)], "SV", 6)
         half_of_group(0, 1, "SVSV")
         quantise_tokens(4, (0, 1))
         half_of_group(1, 1, "SVSV")
         transposes(5, "SVSV")
-        half_of_group(2, 1, "SVSV")
         quantise_tokens(5, (0, 1))
+        half_of_group(2, 1, "SVSV")
         fill(3, 0, [(0, 1), (1, 1)], "SV")
         store_rows(3, 0, 0, 2)
         fill(3, 2, [(2, 1), (3, 1)], "SV")
         store_rows(3, 2, 2, 2)
         transposes(6, "SVSV")
-        for s in range(4, GROUPS):
-            if 5 < s + 1 < GROUPS:
-                quantise_tokens(s + 1, (0, 1))
-            for j in range(4):
-                fill(s, j - j % 2, [(j, 0), (j, 1)], "SV")
-                if s in (7,):
-                    store_rows(s, j - j % 2, j, 1)
-                elif j % 2 == 1:
-                    store_rows(s, j - 1, j - 1, 2)
-                if s == 4 and j == 3:
-                    transposes(7, "SVSV")
+        quantise_tokens(6, (0, 1))
+        fill(4, 0, [(0, 0), (0, 1)], "SV")
+        fill(4, 0, [(1, 0), (1, 1)], "SV")
+        store_rows(4, 0, 0, 2)
+        fill(4, 2, [(2, 0), (2, 1)], "SV")
+        fill(4, 2, [(3, 0), (3, 1)], "SV")
+        store_rows(4, 2, 2, 2)
+        transposes(7, "SVSV")
+        quantise_tokens(7, (0, 1))
+        fill(5, 0, [(0, 0), (0, 1)], "SV")
+        store_rows(5, 0, 0, 1)
+        fill(5, 0, [(1, 0), (1, 1)], "SV")
+        store_rows(5, 0, 1, 1)
+        fill(5, 2, [(2, 0), (2, 1)], "SV")
+        store_rows(5, 2, 2, 1)
+        fill(5, 2, [(3, 0), (3, 1)], "SV")
+        store_rows(5, 2, 3, 1)
+        fill(6, 0, [(0, 0), (0, 1)], "SV")
+        fill(6, 0, [(1, 0), (1, 1)], "SV")
+        store_rows(6, 0, 0, 2)
+        fill(6, 2, [(2, 0), (2, 1)], "SV")
+        fill(6, 2, [(3, 0), (3, 1)], "SV")
+        store_rows(6, 2, 2, 2)
+        fill(7, 0, [(0, 0), (0, 1)], "SV")
+        fill(7, 0, [(1, 0), (1, 1)], "SV")
+        store_rows(7, 0, 0, 2)
+        fill(7, 2, [(2, 0), (2, 1)], "SV")
+        store_rows(7, 2, 2, 1)
+        fill(7, 2, [(3, 0), (3, 1)], "SV")
+        store_rows(7, 2, 3, 1)

@@ -312,12 +312,11 @@ def tile_bitlinear_t_kernel(tc, x, weight, bias, grad_out, out):
             code_tiles(s)
         exceeds()
         transposes(0, "SSSS", 0)
-        keep_busy(2, 4)
+        keep_busy(3, 4)
         load_tokens(6)
         sign_half_1(3)
         ternarise_00()
         transposes(1, "SSSS", 4)
-        keep_busy(1, 0)
         quantise_tokens(0, (0,), (0, 1))
         quantise_q(0, 0)
         quantise_tokens(0, (0,), (2, 3))
@@ -341,16 +340,17 @@ def tile_bitlinear_t_kernel(tc, x, weight, bias, grad_out, out):
         quantise_tokens(1, (0, 1), (2, 3))
         half_products(1, 0, early + [product(1, 2, 0, 6), product(1, 3, 0, 7)], "SSSS")
         load_tokens(7)
-        transposes(3, "SSSS", 0)
+        turned = turn(3, 0)
         quantise_tokens(2, (0, 1))
         ternarise(0, 1)
+        lay_out(3, turned, "SSSV")
         half_of_group(2, 0, "SSSS", 4)
         turned = turn(4, 0)
         ternarise(1, 1)
         quantise_tokens(3, (0, 1))
         quantise_q(0, 1)
         quantise_q(1, 1)
-        lay_out(4, turned, "VVVV")
+        lay_out(4, turned, "SVSV")
         fill(3, 0, [(0, 0), (1, 0)], "SV", 4)
         fill(3, 2, [(2, 0), (3, 0)], "SV", 6)
         half_of_group(0, 1, "SVSV")

@@ -356,41 +356,21 @@ def tile_bitlinear_t_kernel(tc, x, weight, bias, grad_out, out):
         half_of_group(0, 1, "SVSV")
         quantise_tokens(4, (0, 1))
         half_of_group(1, 1, "SVSV")
-        transposes(5, "SVSV")
-        quantise_tokens(5, (0, 1))
         half_of_group(2, 1, "SVSV")
         fill(3, 0, [(0, 1), (1, 1)], "SV")
         store_rows(3, 0, 0, 2)
         fill(3, 2, [(2, 1), (3, 1)], "SV")
         store_rows(3, 2, 2, 2)
-        transposes(6, "SVSV")
-        quantise_tokens(6, (0, 1))
-        fill(4, 0, [(0, 0), (0, 1)], "SV")
-        fill(4, 0, [(1, 0), (1, 1)], "SV")
-        store_rows(4, 0, 0, 2)
-        fill(4, 2, [(2, 0), (2, 1)], "SV")
-        fill(4, 2, [(3, 0), (3, 1)], "SV")
-        store_rows(4, 2, 2, 2)
-        transposes(7, "SVSV")
-        quantise_tokens(7, (0, 1))
-        fill(5, 0, [(0, 0), (0, 1)], "SV")
-        store_rows(5, 0, 0, 1)
-        fill(5, 0, [(1, 0), (1, 1)], "SV")
-        store_rows(5, 0, 1, 1)
-        fill(5, 2, [(2, 0), (2, 1)], "SV")
-        store_rows(5, 2, 2, 1)
-        fill(5, 2, [(3, 0), (3, 1)], "SV")
-        store_rows(5, 2, 3, 1)
-        fill(6, 0, [(0, 0), (0, 1)], "SV")
-        fill(6, 0, [(1, 0), (1, 1)], "SV")
-        store_rows(6, 0, 0, 2)
-        fill(6, 2, [(2, 0), (2, 1)], "SV")
-        fill(6, 2, [(3, 0), (3, 1)], "SV")
-        store_rows(6, 2, 2, 2)
-        fill(7, 0, [(0, 0), (0, 1)], "SV")
-        fill(7, 0, [(1, 0), (1, 1)], "SV")
-        store_rows(7, 0, 0, 2)
-        fill(7, 2, [(2, 0), (2, 1)], "SV")
-        store_rows(7, 2, 2, 1)
-        fill(7, 2, [(3, 0), (3, 1)], "SV")
-        store_rows(7, 2, 3, 1)
+        for s in range(4, GROUPS):
+            for j in range(4):
+                fill(s, j // 2 * 2, [(j, 0), (j, 1)], "SV")
+                if s >= GROUPS - 2:
+                    store_rows(s, j // 2 * 2, j, 1)
+                elif j % 2 == 1:
+                    store_rows(s, j - 1, j - 1, 2)
+                if s + 1 < GROUPS:
+                    if j == 0:
+                        transposes(s + 1, "SVSV")
+                        quantise_tokens(s + 1, (0, 1), (0, 1))
+                    elif j == 1:
+                        quantise_tokens(s + 1, (0, 1), (2, 3))

from contextlib import ExitStack

import concourse.mybir as mybir
from concourse.masks import make_identity

F32 = mybir.dt.float32
BF16 = mybir.dt.bfloat16
I32 = mybir.dt.int32
U32 = mybir.dt.uint32
U8 = mybir.dt.uint8
E4M3X4 = mybir.dt.float8_e4m3fn_x4
E5M2X4 = mybir.dt.float8_e5m2_x4
ALU = mybir.AluOpType
ACTF = mybir.ActivationFunctionType

P = 128
TOKENS = 4096
N_CON = 1024
K_OUT = 1024
THRESHOLD = 0.05
EPS = 1e-6

FLOPS = 2 * TOKENS * N_CON * K_OUT
BYTES = 2 * N_CON * K_OUT + 2 * TOKENS * N_CON + 4 * TOKENS * K_OUT

GROUPS = TOKENS // 512
HALF = 512
G_RESIDENT = 6

SUM_COLS = 256

ABS_BITS = 0x7FFF7FFF
SIGN_BITS = -0x7FFF8000
ONE_BITS = 0x3F803F80

CODE_PAD = 48
SCALE_SLOT = 256


def tile_bitlinear_t_kernel(tc, x, weight, bias, grad_out, out):
    nc = tc.nc
    with ExitStack() as ctx:
        const = ctx.enter_context(tc.tile_pool(name="const", bufs=1))
        g_pool = ctx.enter_context(tc.tile_pool(name="g_pool", bufs=G_RESIDENT))
        gg_pool = ctx.enter_context(tc.tile_pool(name="gg_pool", bufs=3))
        gc_pool = ctx.enter_context(tc.tile_pool(name="gc_pool", bufs=GROUPS))
        qw_pool = ctx.enter_context(tc.tile_pool(name="qw_pool", bufs=2))
        st_pool = ctx.enter_context(tc.tile_pool(name="st_pool", bufs=7))
        psum = ctx.enter_context(tc.psum_pool(name="psum", bufs=1))
        ctx.enter_context(tc.manual_schedule())

        ident = const.tile([P, P], F32, name="ident")
        ones = const.tile([P, P], BF16, name="ones")
        warm = const.tile([P, 1], F32, name="warm")
        busy = const.tile([P, HALF], BF16, name="busy")
        parts_sum = const.tile([P, SUM_COLS], F32, name="parts_sum")
        mean_t = const.tile([P, 1], F32, name="mean_t")
        thr = const.tile([P, 1], F32, name="thr")
        w_sb = [st_pool.tile([P, 4 * K_OUT], BF16, name="w_sb%d" % g, tag="staged") for g in range(2)]
        a_sb = [const.tile([P, 4 * K_OUT], BF16, name="a_sb%d" % g) for g in range(2)]
        a_i = const.tile([P, 4 * HALF], BF16, name="a_i")
        s_i = {g: const.tile([P, 4 * HALF], BF16, name="s_i%d" % g) for g in range(2)}
        s_sb = {g: const.tile([P, 4 * HALF], BF16, name="s_sb%d" % g) for g in range(2)}
        q_codes = const.tile([P, 2 * K_OUT], U32, name="q_codes", align_bytes=256)
        q_scales = const.tile([P, 2 * K_OUT], U8, name="q_scales", align_bytes=256)

        nc.vector.memset(warm[:], 0.0)
        nc.scalar.activation(out=warm[:], in_=warm[:], func=ACTF.Sign)
        nc.vector.memset(busy[:], 1.0)
        nc.vector.memset(ones[:], 1.0)
        make_identity(nc, ident[:])

        g_sb = {}
        g_t = {}
        g_codes = {}
        g_scales = {}
        row_tile = {}
        q_bf = {}

        bank_of = {"next": 0}

        def bank(place=None):
            if place is None:
                place = bank_of["next"] % 8
                bank_of["next"] += 1
            tile = psum.tile([P, HALF], F32, name="bank%d" % place, tag="bank%d" % place)
            return tile

        def load_weight(t, rows):
            k, base = t // 2, t % 2
            nc.sync.dma_start(
                out=w_sb[t // 4][:, (t % 4) * K_OUT : (t % 4 + rows) * K_OUT].rearrange("p (e c) -> p e c", e=rows),
                in_=weight[256 * k : 256 * (k + 1), :].rearrange("(p e) c -> p e c", e=2)[:, base : base + rows, :],
            )

        def load_tokens(s):
            g_sb[s] = g_pool.tile([P, 4 * N_CON], BF16, name="g_sb%d" % s, tag="g_sb")
            nc.sync.dma_start(
                out=g_sb[s][:],
                in_=grad_out[512 * s : 512 * (s + 1), :].rearrange("(p j) n -> p (j n)", j=4),
            )

        def take_abs(t, rows):
            cols = slice((t % 4) * K_OUT, (t % 4 + rows) * K_OUT)
            nc.vector.tensor_scalar(
                out=a_sb[t // 4][:, cols].bitcast(I32), in0=w_sb[t // 4][:, cols].bitcast(I32),
                scalar1=ABS_BITS, scalar2=None, op0=ALU.bitwise_and,
            )

        def add_up(t, rows):
            for c in range((t % 4) * K_OUT, (t % 4 + rows) * K_OUT, SUM_COLS):
                nc.tensor.matmul(
                    out=total[:, 0:SUM_COLS], lhsT=ones[:], rhs=a_sb[t // 4][:, c : c + SUM_COLS],
                    start=(t == 0 and c == 0), stop=(t // 4 == 1 and c == 4 * K_OUT - SUM_COLS),
                )

        def keep_busy(n, place):
            idle = bank(place)
            for i in range(n):
                nc.tensor.matmul(out=idle[:], lhsT=ones[:], rhs=busy[:], start=True, stop=True)

        def quarter(tile, h):
            return tile[:].rearrange("p (t c) -> p c t", t=4)[:, h * HALF : (h + 1) * HALF, :]

        def by_word(tile):
            return tile[:].rearrange("p (c t) -> p c t", t=4)

        def sign_bits(dst, src):
            nc.vector.tensor_scalar(
                out=dst, in0=src, scalar1=SIGN_BITS, scalar2=ONE_BITS, op0=ALU.bitwise_and, op1=ALU.bitwise_or,
            )

        def sign_half_1(k):
            g, u = k // 2, k % 2
            sign_bits(
                s_sb[g][:, u * 2 * HALF : (u + 1) * 2 * HALF].bitcast(I32).rearrange("p (e c) -> p e c", e=2),
                w_sb[g][:, u * 2048 : (u + 1) * 2048].bitcast(I32).rearrange("p (e c) -> p e c", e=2)[:, :, HALF // 2 : HALF],
            )

        def threshold():
            nc.vector.tensor_scalar(
                out=parts_sum[:], in0=total[:, 0:SUM_COLS], scalar1=THRESHOLD / (N_CON * K_OUT), scalar2=None,
                op0=ALU.mult, op1=ALU.add, accum_out=mean_t[:],
            )
            sign_half_1(2)
            nc.vector.tensor_scalar(out=thr[:], in0=mean_t[:], scalar1=THRESHOLD * EPS, scalar2=None, op0=ALU.max)

        def q_tile(g, h):
            q_bf[(g, h)] = qw_pool.tile([P, 4 * HALF], BF16, name="q_bf%d%d" % (g, h), tag="q_bf", align_bytes=64)
            return q_bf[(g, h)]

        def exceeds():
            nc.vector.tensor_scalar(out=a_i[:], in0=a_i[:], scalar1=thr[:, 0:1], scalar2=None, op0=ALU.is_gt)

        def ternarise_00():
            nc.vector.tensor_tensor(out=q_tile(0, 0)[:], in0=a_i[:], in1=s_i[0][:], op=ALU.mult)

        def ternarise(g, h):
            nc.vector.scalar_tensor_tensor(
                out=by_word(q_tile(g, h)),
                in0=quarter(a_sb[g], h),
                scalar=thr[:, 0:1],
                in1=by_word(s_i[g]) if h == 0 else s_sb[g][:].rearrange("p (t c) -> p c t", t=4),
                op0=ALU.is_gt,
                op1=ALU.mult,
            )

        def q_cols(g, h):
            return slice(g * K_OUT + h * HALF, g * K_OUT + (h + 1) * HALF)

        def quantise_q(g, h):
            nc.vector.quantize_mx(
                out=q_codes[:, q_cols(g, h)].bitcast(E4M3X4),
                scales=q_scales[:, q_cols(g, h)],
                in_=q_bf[(g, h)][:],
            )

        def copy_out(engine, dst, src):
            if engine == "S":
                nc.scalar.copy(out=dst, in_=src)
            else:
                nc.vector.tensor_copy(out=dst, in_=src)

        def turn(s, first=None):
            words = g_sb[s][:].bitcast(F32)
            banks = []
            for j in range(4):
                tp = bank(None if first is None else first + j)
                for k in range(4):
                    nc.tensor.transpose(
                        out=tp[:, k * 128 : (k + 1) * 128],
                        in_=words[:, j * 512 + k * 128 : j * 512 + (k + 1) * 128],
                        identity=ident[:],
                    )
                banks.append(tp)
            return banks

        def lay_out(s, banks, engines):
            g_t[s] = gg_pool.tile([P, 4 * N_CON], BF16, name="g_t%d" % s, tag="g_t", align_bytes=64)
            for j in range(4):
                copy_out(
                    engines[j],
                    g_t[s][:].bitcast(F32)[:, j * 512 : (j + 1) * 512].rearrange("p (g m u) -> p g m u", g=2, u=2),
                    banks[j][:].rearrange("p (g u m) -> p g m u", g=2, u=2),
                )

        def transposes(s, engines, first=None):
            lay_out(s, turn(s, first), engines)

        def code_cols(j, g):
            return slice(CODE_PAD + 128 * (2 * j + g), CODE_PAD + 128 * (2 * j + g + 1))

        def scale_cols(j, g):
            return slice(SCALE_SLOT * (2 * j + g), SCALE_SLOT * (2 * j + g) + 128)

        def code_tiles(s):
            g_codes[s] = gc_pool.tile([P, CODE_PAD + 1024], U32, name="g_codes%d" % s, tag="g_codes", align_bytes=256)
            g_scales[s] = gc_pool.tile([P, 8 * SCALE_SLOT], U8, name="g_scales%d" % s, tag="g_scales", align_bytes=256)

        def quantise_tokens(s, passes, tiles=range(4)):
            for j in tiles:
                for g in passes:
                    nc.vector.quantize_mx(
                        out=g_codes[s][:, code_cols(j, g)].bitcast(E5M2X4),
                        scales=g_scales[s][:, scale_cols(j, g)],
                        in_=g_t[s][:, 512 * (2 * j + g) : 512 * (2 * j + g + 1)],
                    )

        def mx_pass(s, j, h, g, acc):
            nc.tensor.matmul_mx(
                out=acc[:],
                lhsT=g_codes[s][:, code_cols(j, g)].bitcast(E5M2X4),
                lhsT_scale=g_scales[s][:, scale_cols(j, g)],
                rhs=q_codes[:, q_cols(g, h)].bitcast(E4M3X4),
                rhs_scale=q_scales[:, q_cols(g, h)],
                start=(g == 0),
                stop=(g == 1),
            )

        def product(s, j, h, place=None):
            acc = bank(place)
            for g in range(2):
                mx_pass(s, j, h, g, acc)
            return acc

        def group_rows(s):
            return out[512 * s : 512 * (s + 1), :].rearrange("(p j) c -> p j c", j=4)

        def half_products(s, h, accs, engines):
            staged = st_pool.tile([P, 4 * HALF], F32, name="staged_h", tag="staged")
            for j in range(4):
                copy_out(engines[j], staged[:, j * HALF : (j + 1) * HALF], accs[j][:])
                if j % 2 == 1:
                    nc.sync.dma_start(
                        out=group_rows(s)[:, j - 1 : j + 1, h * HALF : (h + 1) * HALF],
                        in_=staged[:, (j - 1) * HALF : (j + 1) * HALF].rearrange("p (r c) -> p r c", r=2),
                    )

        def half_of_group(s, h, engines, first=None):
            half_products(s, h, [product(s, j, h, None if first is None else first + j) for j in range(4)], engines)

        def fill(s, j, parts, engines, first=None):
            if (s, j) not in row_tile:
                row_tile[(s, j)] = st_pool.tile([P, 2 * K_OUT], F32, name="staged_w", tag="staged")
            for i, (jj, h) in enumerate(parts):
                c = (jj - j) * K_OUT + h * HALF
                copy_out(engines[i], row_tile[(s, j)][:, c : c + HALF], product(s, jj, h, None if first is None else first + i)[:])

        def store_rows(s, j, first, tiles):
            c = (first - j) * K_OUT
            nc.sync.dma_start(
                out=group_rows(s)[:, first : first + tiles, :],
                in_=row_tile[(s, j)][:, c : c + tiles * K_OUT].rearrange("p (r c) -> p r c", r=tiles),
            )

        def two_tiles(s, j, engines):
            fill(s, j, [(j, 0), (j, 1), (j + 1, 0), (j + 1, 1)], engines)
            store_rows(s, j, j, 2)

        pieces = [(0, 2), (2, 2), (4, 2), (6, 1), (7, 1)]
        for t, rows in pieces:
            load_weight(t, rows)
        for s in range(G_RESIDENT):
            load_tokens(s)
        keep_busy(6, 4)
        total = bank(7)
        for t in range(2):
            take_abs(t, 1)
            add_up(t, 1)
        for t in range(2, 4):
            take_abs(t, 1)
            add_up(t, 1)
        nc.scalar.copy(out=by_word(a_i), in_=quarter(w_sb[0], 0))
        sign_half_1(0)
        for t in range(4, 6):
            take_abs(t, 1)
            add_up(t, 1)
        take_abs(6, 1)
        add_up(6, 1)
        sign_half_1(1)
        take_abs(7, 1)
        add_up(7, 1)
        nc.scalar.activation(out=by_word(s_i[1]), in_=quarter(w_sb[1], 0), func=ACTF.Sign)
        sign_bits(s_i[0][:].bitcast(I32), a_i[:].bitcast(I32))
        nc.vector.tensor_scalar(
            out=a_i[:].bitcast(I32), in0=a_i[:].bitcast(I32), scalar1=ABS_BITS, scalar2=None, op0=ALU.bitwise_and,
        )
        threshold()

        keep_busy(2, 4)
        for s in range(GROUPS):
            code_tiles(s)
        exceeds()
        transposes(0, "SSSS", 0)
        keep_busy(3, 4)
        load_tokens(6)
        sign_half_1(3)
        ternarise_00()
        transposes(1, "SSSS", 4)
        quantise_tokens(0, (0,), (0, 1))
        quantise_q(0, 0)
        quantise_tokens(0, (0,), (2, 3))
        accs = [bank(j) for j in range(4)]
        for j in range(4):
            mx_pass(0, j, 0, 0, accs[j])
        transposes(2, "SSSS", 4)
        ternarise(1, 0)
        quantise_tokens(1, (0,), (0, 1))
        quantise_q(1, 0)
        quantise_tokens(0, (1,))
        early = [bank(4), bank(5)]
        for j in range(2):
            mx_pass(1, j, 0, 0, early[j])
        for j in range(4):
            mx_pass(0, j, 0, 1, accs[j])
        quantise_tokens(1, (1,), (0, 1))
        half_products(0, 0, accs, "SSSS")
        for j in range(2):
            mx_pass(1, j, 0, 1, early[j])
        quantise_tokens(1, (0, 1), (2, 3))
        half_products(1, 0, early + [product(1, 2, 0, 6), product(1, 3, 0, 7)], "SSSS")
        load_tokens(7)
        turned = turn(3, 0)
        quantise_tokens(2, (0, 1))
        ternarise(0, 1)
        lay_out(3, turned, "SSSV")
        half_of_group(2, 0, "SSSS", 4)
        turned = turn(4, 0)
        ternarise(1, 1)
        quantise_tokens(3, (0, 1))
        quantise_q(0, 1)
        quantise_q(1, 1)
        lay_out(4, turned, "SVSV")
        fill(3, 0, [(0, 0), (1, 0)], "SV", 4)
        fill(3, 2, [(2, 0), (3, 0)], "SV", 6)
        half_of_group(0, 1, "SVSV")
        quantise_tokens(4, (0, 1))
        half_of_group(1, 1, "SVSV")
        half_of_group(2, 1, "SVSV")
        fill(3, 0, [(0, 1), (1, 1)], "SV")
        store_rows(3, 0, 0, 2)
        fill(3, 2, [(2, 1), (3, 1)], "SV")
        store_rows(3, 2, 2, 2)
        for s in range(4, GROUPS):
            for j in range(4):
                fill(s, j // 2 * 2, [(j, 0), (j, 1)], "SV")
                if s >= GROUPS - 2:
                    store_rows(s, j // 2 * 2, j, 1)
                elif j % 2 == 1:
                    store_rows(s, j - 1, j - 1, 2)
                if s + 1 < GROUPS:
                    if j == 0:
                        transposes(s + 1, "SVSV")
                        quantise_tokens(s + 1, (0, 1), (0, 1))
                    elif j == 1:
                        quantise_tokens(s + 1, (0, 1), (2, 3))
